import numpy as np
import ml_dtypes


def mxq(x, axis, fmt="e4m3"):
    dtype, down = {"e4m3": (ml_dtypes.float8_e4m3fn, 7), "e5m2": (ml_dtypes.float8_e5m2, 14)}[fmt]
    v = np.moveaxis(np.asarray(x, np.float32).astype(ml_dtypes.bfloat16).astype(np.float64), axis, -1)
    blocks = v.reshape(v.shape[:-1] + (-1, 32))
    amax = np.abs(blocks).max(-1, keepdims=True)
    byte = np.maximum(np.where(amax > 0, np.frexp(amax)[1] - 1 + 127, 0) - down, 1)
    scale = np.exp2(byte - 127.0)
    codes = (blocks / scale).astype(np.float32).astype(dtype).astype(np.float64)
    return np.moveaxis((codes * scale).reshape(v.shape), -1, axis)


WIDE = False


def mx_kscale(k):
    if not WIDE:
        return np.ones(k)
    levels = np.array([10, -10, 5, -5, 0])
    a = np.random.permutation(np.resize(levels, k // 512 * 4)).reshape(k // 512, 4)
    idx = np.arange(k)
    return np.exp2(a[idx // 512, idx % 128 // 32])


BF16 = ml_dtypes.bfloat16


def bf(x):
    return np.asarray(x, np.float32).astype(BF16)


def f64(x):
    return np.asarray(x).astype(np.float64)


E2M1 = np.array([0.0, 0.5, 1.0, 1.5, 2.0, 3.0, 4.0, 6.0, -0.0, -0.5, -1.0, -1.5, -2.0, -3.0, -4.0, -6.0])


def pack_weight(w, fmt):
    k, n = w.shape
    w = f64(bf(w)).reshape(k // 32, 32, n)
    amax = np.abs(w).max(1)
    if fmt == "e4m3":
        byte = np.frexp(amax)[1] - 1 + 127 - 7
    else:
        mant, ex = np.frexp(amax / 6.0)
        byte = np.where(mant > 0.5, ex, ex - 1) + 127
    byte = np.clip(np.where(amax > 0, byte, 1), 1, 254)
    scaled = (w * np.exp2(127.0 - byte)[:, None, :]).reshape(k, n).astype(np.float32)
    by_word = np.ascontiguousarray(scaled.reshape(k // 512, 128, 4, n).transpose(0, 1, 3, 2))
    if fmt == "e4m3":
        words = by_word.astype(ml_dtypes.float8_e4m3fn).view(np.uint8)
    else:
        c = by_word.astype(ml_dtypes.float4_e2m1fn).view(np.uint8) & 0xF
        words = c[..., 0::2] | (c[..., 1::2] << 4)
    return np.ascontiguousarray(words), np.ascontiguousarray(byte.astype(np.uint8).reshape(k // 512, 16, n))


def unpack_weight(words, scales, fmt):
    g, p, n, _ = words.shape
    if fmt == "e4m3":
        vals = np.ascontiguousarray(words).view(ml_dtypes.float8_e4m3fn).astype(np.float64)
    else:
        nib = np.empty((g, p, n, 4), np.uint8)
        nib[..., 0::2] = words & 0xF
        nib[..., 1::2] = words >> 4
        vals = E2M1[nib]
    vals = vals * np.repeat(np.exp2(scales.astype(np.float64) - 127.0), 8, axis=1)[..., None]
    return vals.transpose(0, 1, 3, 2).reshape(g * 512, n)


B, C, L = 1, 16, 32768
LEVEL = 3
NODES = 2 ** LEVEL
D = L // NODES
INV_SQRT2 = 0.7071067811865476


def haar_wpt(x, level):
    c = x[:, :, None, :]
    for _ in range(level):
        Bn, Cn, N, n = c.shape
        y = c.reshape(Bn, Cn, N, n // 2, 2)
        a = (y[..., 0] + y[..., 1]) * INV_SQRT2
        d = (y[..., 0] - y[..., 1]) * INV_SQRT2
        c = np.stack([a, d], axis=3).reshape(Bn, Cn, N * 2, n // 2)
    return c


def haar_iwpt(c, level):
    for _ in range(level):
        a = c[:, :, 0::2, :]
        d = c[:, :, 1::2, :]
        even = (a + d) * INV_SQRT2
        odd = (a - d) * INV_SQRT2
        Bn, Cn, N2, n = even.shape
        c = np.stack([even, odd], axis=-1).reshape(Bn, Cn, N2, 2 * n)
    return c[:, :, 0, :]


def setup_inputs():
    s = mx_kscale(D)
    x = bf(np.random.standard_normal((B, C, L)) * np.repeat(s, NODES))
    w = np.random.standard_normal((D, D)) / np.sqrt(D) / s[None, :]
    words, scales = pack_weight(np.ascontiguousarray(w.T), "e4m3")
    b = bf(np.random.standard_normal(D) * 0.1)
    threshold = bf(np.random.uniform(0.08, 0.12, 1))
    return {"x": x,
            "W_words": words,
            "W_scales": scales,
            "b": b,
            "threshold": threshold}


def reference(x, W_words, W_scales, b, threshold):
    x = f64(x)
    coeffs = haar_wpt(x, LEVEL)
    z = (mxq(coeffs, 3, "e4m3") @ unpack_weight(W_words, W_scales, "e4m3")) + f64(b)
    gate = 1.0 / (1.0 + np.exp(-z))
    gated = coeffs * gate
    gated = np.where(np.abs(gated) < f64(threshold), 0.0, gated)
    recon = haar_iwpt(gated, LEVEL)
    return recon + x

@@ -1,0 +1,312 @@
+import math
+from contextlib import ExitStack
+
+import concourse.mybir as mybir
+from concourse.masks import make_identity
+
+F32 = mybir.dt.float32
+BF16 = mybir.dt.bfloat16
+I32 = mybir.dt.int32
+U32 = mybir.dt.uint32
+U8 = mybir.dt.uint8
+FP8X4 = mybir.dt.float8_e4m3fn_x4
+ALU = mybir.AluOpType
+ACT = mybir.ActivationFunctionType
+
+P = 128
+D = 4096
+FLOPS = 2 * 128 * 4096 * 4096
+
+
+def tile_waveletgatednet_w_kernel(tc, x, W_words, W_scales, b, threshold, out):
+    nc = tc.nc
+    with ExitStack() as ctx:
+        const = ctx.enter_context(tc.tile_pool(name="const", bufs=1))
+        keep = ctx.enter_context(tc.tile_pool(name="keep", bufs=1))
+        fw = ctx.enter_context(tc.tile_pool(name="fw", bufs=2))
+        fx = ctx.enter_context(tc.tile_pool(name="fx", bufs=4))
+        ep = ctx.enter_context(tc.tile_pool(name="ep", bufs=2))
+        psz = ctx.enter_context(tc.psum_pool(name="psz", bufs=4))
+        pso = ctx.enter_context(tc.psum_pool(name="pso", bufs=2))
+        psf = ctx.enter_context(tc.psum_pool(name="psf", bufs=2))
+        ctx.enter_context(tc.manual_schedule())
+
+        planes = keep.tile([P, 2, D], U8, align_bytes=64)
+        xt = keep.tile([P, 4, 1024], BF16)
+        ww = keep.tile([P, 8, D], U32, align_bytes=64)
+        cw = keep.tile([P, 8, P], U32, align_bytes=64)
+        cs = keep.tile([P, 8, P], U8, align_bytes=64)
+        ut = keep.tile([P, 8, 512], F32)
+
+        nc.vector.memset(planes[:].rearrange("p a n -> p (a n)").bitcast(I32), 0)
+        btile = const.tile([P, P], BF16)
+        nc.vector.memset(btile[:], 0.0)
+        warm = const.tile([P, 1], F32)
+        nc.vector.memset(warm[:], 0.0)
+
+        xv = x.rearrange("o c (h j w) -> (o c) j h w", h=4, j=8)
+        ov = out.rearrange("o c (h j w) -> (o c) j h w", h=4, j=8)
+        for dh in range(4):
+            nc.sync.dma_start(out=xt[:, dh, :], in_=xv[:, :, dh, :])
+        nc.scalar.dma_start(out=btile[0:32, :], in_=b.rearrange("(r c) -> r c", c=P))
+        thr_b = const.tile([P, 1], BF16)
+        nc.scalar.dma_start(out=thr_b[:], in_=threshold.partition_broadcast(P))
+        warm2 = const.tile([P, 1], F32)
+        nc.scalar.activation(out=warm2[:], in_=warm[:], func=ACT.Sigmoid)
+        for a in range(2):
+            for q in range(4):
+                nc.sync.dma_start(
+                    out=planes[32 * q : 32 * q + 16, a, :].bitcast(I32),
+                    in_=W_scales[4 * a : 4 * a + 4, 4 * q : 4 * q + 4, :].bitcast(I32),
+                )
+        w32 = W_words.rearrange("g p n t -> g p (n t)").bitcast(I32)
+        for hc in range(7):
+            cols = slice(512 * hc, 512 * (hc + 1))
+            for gp in range(4):
+                nc.sync.dma_start(
+                    out=ww[:, 2 * gp : 2 * gp + 2, cols].bitcast(I32),
+                    in_=w32[2 * gp : 2 * gp + 2, :, cols].rearrange("g p n -> p g n"),
+                )
+        for g in range(8):
+            nc.sync.dma_start(out=ww[:, g, 3584:4096].bitcast(I32), in_=w32[g, :, 3584:4096])
+
+        row_i = const.tile([P, P], I32)
+        nc.gpsimd.iota(row_i[:], pattern=[[0, P]], base=0, channel_multiplier=1)
+        col_i = const.tile([P, P], I32)
+        nc.gpsimd.iota(col_i[:], pattern=[[1, P]], base=0, channel_multiplier=0)
+        ident_f = const.tile([P, P], F32)
+        make_identity(nc, ident_f[:])
+        ident_b = const.tile([P, P], BF16)
+        make_identity(nc, ident_b[:])
+        both = const.tile([P, P], I32)
+        nc.vector.tensor_tensor(out=both[:], in0=row_i[:], in1=col_i[:], op=ALU.bitwise_and)
+        sh1 = const.tile([P, P], I32)
+        nc.vector.tensor_single_scalar(out=sh1[:], in_=both[:], scalar=1, op=ALU.logical_shift_right)
+        sh2 = const.tile([P, P], I32)
+        nc.vector.tensor_single_scalar(out=sh2[:], in_=both[:], scalar=2, op=ALU.logical_shift_right)
+        nc.vector.tensor_tensor(out=sh1[:], in0=sh1[:], in1=both[:], op=ALU.bitwise_xor)
+        nc.vector.tensor_tensor(out=sh1[:], in0=sh1[:], in1=sh2[:], op=ALU.bitwise_xor)
+        nc.vector.tensor_single_scalar(out=sh1[:], in_=sh1[:], scalar=1, op=ALU.bitwise_and)
+        diff = const.tile([P, P], I32)
+        nc.vector.tensor_tensor(out=diff[:], in0=row_i[:], in1=col_i[:], op=ALU.bitwise_xor)
+        nc.vector.tensor_single_scalar(out=diff[:], in_=diff[:], scalar=3, op=ALU.logical_shift_right)
+        same = const.tile([P, P], F32)
+        nc.vector.tensor_single_scalar(out=same[:], in_=diff[:], scalar=0, op=ALU.is_equal)
+        sign = const.tile([P, P], F32)
+        nc.vector.tensor_scalar(out=sign[:], in0=sh1[:], scalar1=-0.25, scalar2=0.125, op0=ALU.mult, op1=ALU.add)
+        g8 = const.tile([P, P], BF16)
+        nc.vector.tensor_tensor(out=g8[:], in0=same[:], in1=sign[:], op=ALU.mult)
+        tsq = const.tile([P, 1], F32)
+        bt = const.tile([P, 32], F32)
+
+        xw = xt[:].rearrange("p h w -> p (h w)").bitcast(F32)
+        ps1s = {}
+        rws = {}
+        ps2s = {}
+        x3s = {}
+        ps3s = {}
+        grps = {}
+        ps4s = {}
+
+        def stage_a(dh):
+            ps1 = psf.tile([P, 4, P], F32, tag="f", name="ps1")
+            for m in range(4):
+                nc.tensor.transpose(ps1[:, m, :], xw[:, 512 * dh + m : 512 * (dh + 1) : 4], ident_f[:])
+            ps1s[dh] = ps1
+
+        def stage_b(dh):
+            rw = fw.tile([P, 8, 16, 4], F32, name="rw")
+            nc.vector.tensor_copy(out=rw[:], in_=ps1s[dh][:].rearrange("p m (c j) -> p j c m", j=8))
+            rws[dh] = rw
+
+        def stage_c(dh):
+            rb = rws[dh][:].rearrange("p j c m -> p j (c m)").bitcast(BF16)
+            ps2 = psz.tile([P, 8, P], BF16, tag="z", name="ps2")
+            for jj in range(8):
+                nc.tensor.transpose(ps2[:, jj, :], rb[:, jj, :], ident_b[:])
+            ps2s[dh] = ps2
+
+        def stage_d(dh):
+            x3 = fx.tile([P, 1024], BF16, name="x3")
+            nc.scalar.copy(out=x3[:], in_=ps2s[dh][:].rearrange("p j e -> p (j e)"))
+            x3s[dh] = x3
+
+        def stage_e(dh):
+            for gl in range(2):
+                ps3 = pso.tile([P, 4, P], F32, tag="o", name="ps3")
+                for t in range(4):
+                    nc.tensor.matmul(ps3[:, t, :], lhsT=x3s[dh][:, 512 * gl + t : 512 * (gl + 1) : 4], rhs=g8[:], start=True, stop=True)
+                ps3s[(dh, gl)] = ps3
+
+        def stage_f(dh):
+            grp = fw.tile([P, 2, P, 4], BF16, align_bytes=64, name="grp")
+            nc.scalar.activation(out=grp[:, 0], in_=ps3s[(dh, 0)][:].rearrange("p t r -> p r t"), func=ACT.Copy, scale=math.sqrt(8.0))
+            nc.vector.tensor_single_scalar(out=grp[:, 1], in_=ps3s[(dh, 1)][:].rearrange("p t r -> p r t"), scalar=math.sqrt(8.0), op=ALU.mult)
+            grps[dh] = grp
+
+        def stage_q(dh):
+            nc.vector.quantize_mx(
+                out=cw[:, 2 * dh : 2 * dh + 2, :].rearrange("p g r -> p (g r)").bitcast(FP8X4),
+                scales=cs[:, 2 * dh : 2 * dh + 2, :].rearrange("p g r -> p (g r)"),
+                in_=grps[dh][:].rearrange("p g r t -> p (g r t)"),
+            )
+
+        def stage_h(dh):
+            for hl in range(2):
+                ps4 = psz.tile([P, 4, P], F32, tag="z", name="ps4")
+                for jl in range(4):
+                    e0 = (4 * hl + jl) * P
+                    nc.tensor.matmul(ps4[:, jl, :], lhsT=x3s[dh][:, e0 : e0 + P], rhs=g8[:], start=True, stop=True)
+                ps4s[(dh, hl)] = ps4
+
+        def stage_i(dh):
+            for hl in range(2):
+                nc.scalar.copy(
+                    out=ut[:, 2 * dh + hl, :].rearrange("p (c j n) -> p c j n", j=4, n=8),
+                    in_=ps4s[(dh, hl)][:].rearrange("p j (c n) -> p c j n", n=8),
+                )
+
+        for s in range(7):
+            if s < 4:
+                stage_a(s)
+                stage_b(s)
+            if 0 <= s - 3 < 4:
+                stage_q(s - 3)
+            if 0 <= s - 1 < 4:
+                stage_c(s - 1)
+                stage_d(s - 1)
+            if 0 <= s - 2 < 4:
+                stage_e(s - 2)
+                stage_f(s - 2)
+            if s == 3:
+                psb = psz.tile([P, P], BF16, tag="z", name="psb")
+                nc.tensor.transpose(psb[:], btile[:], ident_b[:])
+                nc.vector.tensor_copy(out=bt[:], in_=psb[:, 0:32])
+                nc.vector.scalar_tensor_tensor(out=tsq[:], in0=thr_b[:], scalar=0.125, in1=thr_b[:], op0=ALU.mult, op1=ALU.mult)
+        stage_h(0)
+        stage_i(0)
+
+        zss = {}
+        gates = {}
+        gts = {}
+        sqs = {}
+        y3s = {}
+        pos = {}
+        ots = {}
+
+        def mx(hc):
+            zs = []
+            if hc < 7:
+                zb = psf.tile([P, 4, P], F32, tag="f", name="zb")
+                for jl in range(4):
+                    zs.append(zb[:, jl, :])
+                order = [(g, jl) for jl in range(4) for g in range(8)]
+            else:
+                for jl in range(4):
+                    zt = psz.tile([P, P], F32, tag="z", name="zt")
+                    zs.append(zt[:])
+                order = [(g, jl) for g in range(8) for jl in range(4)]
+            for g, jl in order:
+                if True:
+                    n0 = 512 * hc + P * jl
+                    nc.tensor.matmul_mx(
+                        out=zs[jl],
+                        lhsT=ww[:, g, n0 : n0 + P].bitcast(FP8X4),
+                        lhsT_scale=planes[4 * (g % 4) : P, g // 4, n0 : n0 + P],
+                        rhs=cw[:, g, :].bitcast(FP8X4),
+                        rhs_scale=cs[:, g, :],
+                        start=(g == 0),
+                        stop=(g == 7),
+                    )
+            zss[hc] = zs
+
+        def sig(hc):
+            gate = ep.tile([P, 16, 4, 8], F32, name="gate")
+            for jl in range(4):
+                eb = 4 * hc + jl
+                nc.scalar.activation(
+                    out=gate[:, :, jl, :],
+                    in_=zss[hc][jl].rearrange("p (c n) -> p c n", n=8),
+                    func=ACT.Sigmoid,
+                    bias=bt[:, eb : eb + 1],
+                    scale=1.0,
+                )
+            gates[hc] = gate
+
+        def half(ap4, a):
+            return ap4[:, :, 2 * a : 2 * a + 2, :].rearrange("p c j n -> p c (j n)")
+
+        def prod(hc):
+            gt = ep.tile([P, 16, 4, 8], F32, name="gt")
+            utv = ut[:, hc, :].rearrange("p (c j n) -> p c j n", j=4, n=8)
+            for a in range(2):
+                nc.vector.tensor_tensor(out=half(gt[:], a), in0=half(gates[hc][:], a), in1=half(utv, a), op=ALU.mult)
+            gts[hc] = gt
+
+        def square(hc):
+            sq = ep.tile([P, 16, 4, 8], F32, name="sq")
+            for a in range(2):
+                nc.scalar.activation(out=half(sq[:], a), in_=half(gts[hc][:], a), func=ACT.Square)
+            sqs[hc] = sq
+
+        def select_and_levels(hc):
+            sq = sqs[hc]
+            for a in range(2):
+                nc.vector.scalar_tensor_tensor(
+                    out=half(sq[:], a), in0=half(sq[:], a), scalar=tsq[:, 0:1], in1=half(gts[hc][:], a), op0=ALU.is_ge, op1=ALU.mult
+                )
+            sl = sq[:].rearrange("p c j (r two) -> p (c j r) two", two=2)
+            y1 = ep.tile([P, 2, 128, 2], F32, name="y1")
+            nc.vector.tensor_tensor(out=y1[:, 0].rearrange("p s two -> p (s two)"), in0=sl[:, :, 0], in1=sl[:, :, 1], op=ALU.add)
+            nc.vector.tensor_tensor(out=y1[:, 1].rearrange("p s two -> p (s two)"), in0=sl[:, :, 0], in1=sl[:, :, 1], op=ALU.subtract)
+            y2 = ep.tile([P, 2, 2, 64, 2], F32, name="y2")
+            nc.vector.tensor_tensor(out=y2[:, 0].rearrange("p b s two -> p b (s two)"), in0=y1[:, :, :, 0], in1=y1[:, :, :, 1], op=ALU.add)
+            nc.vector.tensor_tensor(out=y2[:, 1].rearrange("p b s two -> p b (s two)"), in0=y1[:, :, :, 0], in1=y1[:, :, :, 1], op=ALU.subtract)
+            y2v = y2[:].rearrange("p a b (c j) two -> p (a b) c j two", j=4)
+            dh = hc // 2
+            hl = hc % 2
+            if hl == 0:
+                y3n = ep.tile([P, 2, 4, 16, 2, 4], F32, name="y3")
+                y3s[dh] = y3n
+            y3 = y3s[dh]
+            nc.vector.tensor_tensor(out=y3[:, 0, :, :, hl, :], in0=y2v[:, :, :, :, 0], in1=y2v[:, :, :, :, 1], op=ALU.add)
+            nc.vector.tensor_tensor(out=y3[:, 1, :, :, hl, :], in0=y2v[:, :, :, :, 0], in1=y2v[:, :, :, :, 1], op=ALU.subtract)
+
+        def back(dh):
+            y3p = y3s[dh][:].rearrange("p a b c h j -> p (a b) (c h j)")
+            for h in range(2):
+                po = pso.tile([P, 4, P], F32, tag="o", name="po")
+                for il in range(4):
+                    nc.tensor.transpose(po[:, il, :], y3p[:, 4 * h + il, :], ident_f[:])
+                pos[(dh, h)] = po
+
+        def fin(dh):
+            ot = fx.tile([P, P, 8], F32, name="ot")
+            xr = xt[:, dh, :].rearrange("p (e i) -> p e i", i=8)
+            for h in range(2):
+                nc.vector.tensor_tensor(
+                    out=ot[:, :, 4 * h : 4 * h + 4],
+                    in0=pos[(dh, h)][:].rearrange("p i e -> p e i"),
+                    in1=xr[:, :, 4 * h : 4 * h + 4],
+                    op=ALU.add,
+                )
+            ots[dh] = ot
+
+        for hc in range(8):
+            mx(hc)
+            if hc in (0, 2, 4):
+                stage_h(hc // 2 + 1)
+            if hc % 2 == 0 and hc >= 2:
+                back(hc // 2 - 1)
+            sig(hc)
+            prod(hc)
+            square(hc)
+            if hc in (0, 2, 4):
+                stage_i(hc // 2 + 1)
+            if hc % 2 == 0 and hc >= 2:
+                fin(hc // 2 - 1)
+            select_and_levels(hc)
+        back(3)
+        fin(3)
+        for dh in range(4):
+            nc.sync.dma_start(out=ov[:, :, dh, :], in_=ots[dh][:].rearrange("p e i -> p (e i)"))

@@ -26,6 +26,7 @@ def tile_waveletgatednet_w_kernel(tc, x, W_words, W_scales, b, threshold, out):
         fw = ctx.enter_context(tc.tile_pool(name="fw", bufs=2))
         fx = ctx.enter_context(tc.tile_pool(name="fx", bufs=4))
         ep = ctx.enter_context(tc.tile_pool(name="ep", bufs=2))
+        wp = ctx.enter_context(tc.tile_pool(name="wp", bufs=6))
         psz = ctx.enter_context(tc.psum_pool(name="psz", bufs=4))
         pso = ctx.enter_context(tc.psum_pool(name="pso", bufs=2))
         psf = ctx.enter_context(tc.psum_pool(name="psf", bufs=2))
@@ -33,7 +34,7 @@ def tile_waveletgatednet_w_kernel(tc, x, W_words, W_scales, b, threshold, out):
 
         planes = keep.tile([P, 2, D], U8, align_bytes=64)
         xt = keep.tile([P, 4, 1024], BF16)
-        ww = keep.tile([P, 8, D], U32, align_bytes=64)
+        xpl = keep.tile([P, 4, 8, P], F32)
         cw = keep.tile([P, 8, P], U32, align_bytes=64)
         cs = keep.tile([P, 8, P], U8, align_bytes=64)
         ut = keep.tile([P, 8, 512], F32)
@@ -60,20 +61,29 @@ def tile_waveletgatednet_w_kernel(tc, x, W_words, W_scales, b, threshold, out):
                     in_=W_scales[4 * a : 4 * a + 4, 4 * q : 4 * q + 4, :].bitcast(I32),
                 )
         w32 = W_words.rearrange("g p n t -> g p (n t)").bitcast(I32)
-        for hc in range(7):
+        wts = {}
+
+        def load_w(hc):
+            wt = wp.tile([P, 8, 512], U32, align_bytes=64, name="wt")
             cols = slice(512 * hc, 512 * (hc + 1))
-            for gp in range(4):
-                nc.sync.dma_start(
-                    out=ww[:, 2 * gp : 2 * gp + 2, cols].bitcast(I32),
-                    in_=w32[2 * gp : 2 * gp + 2, :, cols].rearrange("g p n -> p g n"),
-                )
-        for g in range(8):
-            nc.sync.dma_start(out=ww[:, g, 3584:4096].bitcast(I32), in_=w32[g, :, 3584:4096])
+            if hc < 7:
+                for gp in range(4):
+                    nc.sync.dma_start(
+                        out=wt[:, 2 * gp : 2 * gp + 2, :].bitcast(I32),
+                        in_=w32[2 * gp : 2 * gp + 2, :, cols].rearrange("g p n -> p g n"),
+                    )
+            else:
+                for g in range(8):
+                    nc.sync.dma_start(out=wt[:, g, :].bitcast(I32), in_=w32[g, :, cols])
+            wts[hc] = wt
+
+        for hc in range(6):
+            load_w(hc)
 
         row_i = const.tile([P, P], I32)
         nc.gpsimd.iota(row_i[:], pattern=[[0, P]], base=0, channel_multiplier=1)
         col_i = const.tile([P, P], I32)
-        nc.gpsimd.iota(col_i[:], pattern=[[1, P]], base=0, channel_multiplier=0)
+        nc.gpsimd.iota(col_i[:], pattern=[[4, 2], [8, 16], [1, 4]], base=0, channel_multiplier=0)
         ident_f = const.tile([P, P], F32)
         make_identity(nc, ident_f[:])
         ident_b = const.tile([P, P], BF16)
@@ -116,8 +126,12 @@ def tile_waveletgatednet_w_kernel(tc, x, W_words, W_scales, b, threshold, out):
 
         def stage_b(dh):
             rw = fw.tile([P, 8, 16, 4], F32, name="rw")
-            nc.vector.tensor_copy(out=rw[:], in_=ps1s[dh][:].rearrange("p m (c j) -> p j c m", j=8))
+            nc.scalar.copy(out=rw[:], in_=ps1s[dh][:].rearrange("p m (c j) -> p j c m", j=8))
             rws[dh] = rw
+            nc.scalar.copy(
+                out=xpl[:, dh].rearrange("p (m e) q -> p m e q", e=2),
+                in_=ps1s[dh][:].rearrange("p m q -> p (m q)").bitcast(BF16).rearrange("p (m q e) -> p m e q", m=4, e=2),
+            )
 
         def stage_c(dh):
             rb = rws[dh][:].rearrange("p j c m -> p j (c m)").bitcast(BF16)
@@ -128,7 +142,7 @@ def tile_waveletgatednet_w_kernel(tc, x, W_words, W_scales, b, threshold, out):
 
         def stage_d(dh):
             x3 = fx.tile([P, 1024], BF16, name="x3")
-            nc.scalar.copy(out=x3[:], in_=ps2s[dh][:].rearrange("p j e -> p (j e)"))
+            nc.vector.tensor_copy(out=x3[:], in_=ps2s[dh][:].rearrange("p j e -> p (j e)"))
             x3s[dh] = x3
 
         def stage_e(dh):
@@ -162,8 +176,8 @@ def tile_waveletgatednet_w_kernel(tc, x, W_words, W_scales, b, threshold, out):
         def stage_i(dh):
             for hl in range(2):
                 nc.scalar.copy(
-                    out=ut[:, 2 * dh + hl, :].rearrange("p (c j n) -> p c j n", j=4, n=8),
-                    in_=ps4s[(dh, hl)][:].rearrange("p j (c n) -> p c j n", n=8),
+                    out=ut[:, 2 * dh + hl, :].rearrange("p (a j n) -> p a j n", j=4, n=4),
+                    in_=ps4s[(dh, hl)][:].rearrange("p j (a n) -> p a j n", n=4),
                 )
 
         for s in range(7):
@@ -190,7 +204,8 @@ def tile_waveletgatednet_w_kernel(tc, x, W_words, W_scales, b, threshold, out):
         gates = {}
         gts = {}
         sqs = {}
-        y3s = {}
+        y2s = {}
+        ngs = {}
         pos = {}
         ots = {}
 
@@ -207,26 +222,25 @@ def tile_waveletgatednet_w_kernel(tc, x, W_words, W_scales, b, threshold, out):
                     zs.append(zt[:])
                 order = [(g, jl) for g in range(8) for jl in range(4)]
             for g, jl in order:
-                if True:
-                    n0 = 512 * hc + P * jl
-                    nc.tensor.matmul_mx(
-                        out=zs[jl],
-                        lhsT=ww[:, g, n0 : n0 + P].bitcast(FP8X4),
-                        lhsT_scale=planes[4 * (g % 4) : P, g // 4, n0 : n0 + P],
-                        rhs=cw[:, g, :].bitcast(FP8X4),
-                        rhs_scale=cs[:, g, :],
-                        start=(g == 0),
-                        stop=(g == 7),
-                    )
+                n0 = 512 * hc + P * jl
+                nc.tensor.matmul_mx(
+                    out=zs[jl],
+                    lhsT=wts[hc][:, g, P * jl : P * jl + P].bitcast(FP8X4),
+                    lhsT_scale=planes[4 * (g % 4) : P, g // 4, n0 : n0 + P],
+                    rhs=cw[:, g, :].bitcast(FP8X4),
+                    rhs_scale=cs[:, g, :],
+                    start=(g == 0),
+                    stop=(g == 7),
+                )
             zss[hc] = zs
 
         def sig(hc):
-            gate = ep.tile([P, 16, 4, 8], F32, name="gate")
+            gate = ep.tile([P, 32, 4, 4], F32, name="gate")
             for jl in range(4):
                 eb = 4 * hc + jl
                 nc.scalar.activation(
                     out=gate[:, :, jl, :],
-                    in_=zss[hc][jl].rearrange("p (c n) -> p c n", n=8),
+                    in_=zss[hc][jl].rearrange("p (a n) -> p a n", n=4),
                     func=ACT.Sigmoid,
                     bias=bt[:, eb : eb + 1],
                     scale=1.0,
@@ -237,14 +251,14 @@ def tile_waveletgatednet_w_kernel(tc, x, W_words, W_scales, b, threshold, out):
             return ap4[:, :, 2 * a : 2 * a + 2, :].rearrange("p c j n -> p c (j n)")
 
         def prod(hc):
-            gt = ep.tile([P, 16, 4, 8], F32, name="gt")
-            utv = ut[:, hc, :].rearrange("p (c j n) -> p c j n", j=4, n=8)
+            gt = ep.tile([P, 32, 4, 4], F32, name="gt")
+            utv = ut[:, hc, :].rearrange("p (a j n) -> p a j n", j=4, n=4)
             for a in range(2):
                 nc.vector.tensor_tensor(out=half(gt[:], a), in0=half(gates[hc][:], a), in1=half(utv, a), op=ALU.mult)
             gts[hc] = gt
 
         def square(hc):
-            sq = ep.tile([P, 16, 4, 8], F32, name="sq")
+            sq = ep.tile([P, 32, 4, 4], F32, name="sq")
             for a in range(2):
                 nc.scalar.activation(out=half(sq[:], a), in_=half(gts[hc][:], a), func=ACT.Square)
             sqs[hc] = sq
@@ -255,45 +269,49 @@ def tile_waveletgatednet_w_kernel(tc, x, W_words, W_scales, b, threshold, out):
                 nc.vector.scalar_tensor_tensor(
                     out=half(sq[:], a), in0=half(sq[:], a), scalar=tsq[:, 0:1], in1=half(gts[hc][:], a), op0=ALU.is_ge, op1=ALU.mult
                 )
-            sl = sq[:].rearrange("p c j (r two) -> p (c j r) two", two=2)
+            sl = sq[:].rearrange("p a j (r two) -> p (a j r) two", two=2)
             y1 = ep.tile([P, 2, 128, 2], F32, name="y1")
             nc.vector.tensor_tensor(out=y1[:, 0].rearrange("p s two -> p (s two)"), in0=sl[:, :, 0], in1=sl[:, :, 1], op=ALU.add)
             nc.vector.tensor_tensor(out=y1[:, 1].rearrange("p s two -> p (s two)"), in0=sl[:, :, 0], in1=sl[:, :, 1], op=ALU.subtract)
-            y2 = ep.tile([P, 2, 2, 64, 2], F32, name="y2")
-            nc.vector.tensor_tensor(out=y2[:, 0].rearrange("p b s two -> p b (s two)"), in0=y1[:, :, :, 0], in1=y1[:, :, :, 1], op=ALU.add)
-            nc.vector.tensor_tensor(out=y2[:, 1].rearrange("p b s two -> p b (s two)"), in0=y1[:, :, :, 0], in1=y1[:, :, :, 1], op=ALU.subtract)
-            y2v = y2[:].rearrange("p a b (c j) two -> p (a b) c j two", j=4)
             dh = hc // 2
             hl = hc % 2
             if hl == 0:
-                y3n = ep.tile([P, 2, 4, 16, 2, 4], F32, name="y3")
-                y3s[dh] = y3n
-            y3 = y3s[dh]
-            nc.vector.tensor_tensor(out=y3[:, 0, :, :, hl, :], in0=y2v[:, :, :, :, 0], in1=y2v[:, :, :, :, 1], op=ALU.add)
-            nc.vector.tensor_tensor(out=y3[:, 1, :, :, hl, :], in0=y2v[:, :, :, :, 0], in1=y2v[:, :, :, :, 1], op=ALU.subtract)
+                y2n = ep.tile([P, 2, 2, 32, 2, 4], F32, name="y2")
+                y2s[dh] = y2n
+            y2 = y2s[dh]
+            y1v = y1[:].rearrange("p b (a j) two -> p b a j two", j=4)
+            nc.vector.tensor_tensor(out=y2[:, 0, :, :, hl, :], in0=y1v[:, :, :, :, 0], in1=y1v[:, :, :, :, 1], op=ALU.add)
+            nc.vector.tensor_tensor(out=y2[:, 1, :, :, hl, :], in0=y1v[:, :, :, :, 0], in1=y1v[:, :, :, :, 1], op=ALU.subtract)
+
+        def planes_of(dh):
+            return y2s[dh][:].rearrange("p x b (v c) h j -> p (x b) v (c h j)", v=2)
+
+        def neg(dh):
+            ng = ep.tile([P, 4, P], F32, name="ng")
+            nc.scalar.activation(out=ng[:], in_=planes_of(dh)[:, :, 1, :], func=ACT.Copy, scale=-1.0)
+            ngs[dh] = ng
 
         def back(dh):
-            y3p = y3s[dh][:].rearrange("p a b c h j -> p (a b) (c h j)")
-            for h in range(2):
+            yv = planes_of(dh)
+            for i2 in range(2):
                 po = pso.tile([P, 4, P], F32, tag="o", name="po")
                 for il in range(4):
-                    nc.tensor.transpose(po[:, il, :], y3p[:, 4 * h + il, :], ident_f[:])
-                pos[(dh, h)] = po
+                    last = yv[:, il, 1, :] if i2 == 0 else ngs[dh][:, il, :]
+                    nc.tensor.matmul(po[:, il, :], lhsT=xpl[:, dh, 4 * i2 + il, :], rhs=ident_f[:], is_transpose=True, start=True, stop=False)
+                    nc.tensor.matmul(po[:, il, :], lhsT=yv[:, il, 0, :], rhs=ident_f[:], is_transpose=True, start=False, stop=False)
+                    nc.tensor.matmul(po[:, il, :], lhsT=last, rhs=ident_f[:], is_transpose=True, start=False, stop=True)
+                pos[(dh, i2)] = po
 
         def fin(dh):
             ot = fx.tile([P, P, 8], F32, name="ot")
-            xr = xt[:, dh, :].rearrange("p (e i) -> p e i", i=8)
-            for h in range(2):
-                nc.vector.tensor_tensor(
-                    out=ot[:, :, 4 * h : 4 * h + 4],
-                    in0=pos[(dh, h)][:].rearrange("p i e -> p e i"),
-                    in1=xr[:, :, 4 * h : 4 * h + 4],
-                    op=ALU.add,
-                )
+            for i2 in range(2):
+                nc.scalar.copy(out=ot[:, :, 4 * i2 : 4 * i2 + 4], in_=pos[(dh, i2)][:].rearrange("p i e -> p e i"))
             ots[dh] = ot
 
         for hc in range(8):
             mx(hc)
+            if hc < 2:
+                load_w(hc + 6)
             if hc in (0, 2, 4):
                 stage_h(hc // 2 + 1)
             if hc % 2 == 0 and hc >= 2:
@@ -306,6 +324,8 @@ def tile_waveletgatednet_w_kernel(tc, x, W_words, W_scales, b, threshold, out):
             if hc % 2 == 0 and hc >= 2:
                 fin(hc // 2 - 1)
             select_and_levels(hc)
+            if hc % 2 == 1:
+                neg(hc // 2)
         back(3)
         fin(3)
         for dh in range(4):

@@ -26,7 +26,6 @@ def tile_waveletgatednet_w_kernel(tc, x, W_words, W_scales, b, threshold, out):
         fw = ctx.enter_context(tc.tile_pool(name="fw", bufs=2))
         fx = ctx.enter_context(tc.tile_pool(name="fx", bufs=4))
         ep = ctx.enter_context(tc.tile_pool(name="ep", bufs=2))
-        wp = ctx.enter_context(tc.tile_pool(name="wp", bufs=6))
         psz = ctx.enter_context(tc.psum_pool(name="psz", bufs=4))
         pso = ctx.enter_context(tc.psum_pool(name="pso", bufs=2))
         psf = ctx.enter_context(tc.psum_pool(name="psf", bufs=2))
@@ -34,7 +33,7 @@ def tile_waveletgatednet_w_kernel(tc, x, W_words, W_scales, b, threshold, out):
 
         planes = keep.tile([P, 2, D], U8, align_bytes=64)
         xt = keep.tile([P, 4, 1024], BF16)
-        xpl = keep.tile([P, 4, 8, P], F32)
+        ww = keep.tile([P, 8, D], U32, align_bytes=64)
         cw = keep.tile([P, 8, P], U32, align_bytes=64)
         cs = keep.tile([P, 8, P], U8, align_bytes=64)
         ut = keep.tile([P, 8, 512], F32)
@@ -55,35 +54,26 @@ def tile_waveletgatednet_w_kernel(tc, x, W_words, W_scales, b, threshold, out):
         warm2 = const.tile([P, 1], F32)
         nc.scalar.activation(out=warm2[:], in_=warm[:], func=ACT.Sigmoid)
         for a in range(2):
-            for q in range(4):
+            for q in (0, 2, 1, 3):
                 nc.sync.dma_start(
                     out=planes[32 * q : 32 * q + 16, a, :].bitcast(I32),
                     in_=W_scales[4 * a : 4 * a + 4, 4 * q : 4 * q + 4, :].bitcast(I32),
                 )
         w32 = W_words.rearrange("g p n t -> g p (n t)").bitcast(I32)
-        wts = {}
-
-        def load_w(hc):
-            wt = wp.tile([P, 8, 512], U32, align_bytes=64, name="wt")
+        for hc in range(7):
             cols = slice(512 * hc, 512 * (hc + 1))
-            if hc < 7:
-                for gp in range(4):
-                    nc.sync.dma_start(
-                        out=wt[:, 2 * gp : 2 * gp + 2, :].bitcast(I32),
-                        in_=w32[2 * gp : 2 * gp + 2, :, cols].rearrange("g p n -> p g n"),
-                    )
-            else:
-                for g in range(8):
-                    nc.sync.dma_start(out=wt[:, g, :].bitcast(I32), in_=w32[g, :, cols])
-            wts[hc] = wt
-
-        for hc in range(6):
-            load_w(hc)
+            for gp in range(4):
+                nc.sync.dma_start(
+                    out=ww[:, 2 * gp : 2 * gp + 2, cols].bitcast(I32),
+                    in_=w32[2 * gp : 2 * gp + 2, :, cols].rearrange("g p n -> p g n"),
+                )
+        for g in range(8):
+            nc.sync.dma_start(out=ww[:, g, 3584:4096].bitcast(I32), in_=w32[g, :, 3584:4096])
 
         row_i = const.tile([P, P], I32)
         nc.gpsimd.iota(row_i[:], pattern=[[0, P]], base=0, channel_multiplier=1)
         col_i = const.tile([P, P], I32)
-        nc.gpsimd.iota(col_i[:], pattern=[[4, 2], [8, 16], [1, 4]], base=0, channel_multiplier=0)
+        nc.gpsimd.iota(col_i[:], pattern=[[1, P]], base=0, channel_multiplier=0)
         ident_f = const.tile([P, P], F32)
         make_identity(nc, ident_f[:])
         ident_b = const.tile([P, P], BF16)
@@ -126,12 +116,8 @@ def tile_waveletgatednet_w_kernel(tc, x, W_words, W_scales, b, threshold, out):
 
         def stage_b(dh):
             rw = fw.tile([P, 8, 16, 4], F32, name="rw")
-            nc.scalar.copy(out=rw[:], in_=ps1s[dh][:].rearrange("p m (c j) -> p j c m", j=8))
+            nc.vector.tensor_copy(out=rw[:], in_=ps1s[dh][:].rearrange("p m (c j) -> p j c m", j=8))
             rws[dh] = rw
-            nc.scalar.copy(
-                out=xpl[:, dh].rearrange("p (m e) q -> p m e q", e=2),
-                in_=ps1s[dh][:].rearrange("p m q -> p (m q)").bitcast(BF16).rearrange("p (m q e) -> p m e q", m=4, e=2),
-            )
 
         def stage_c(dh):
             rb = rws[dh][:].rearrange("p j c m -> p j (c m)").bitcast(BF16)
@@ -142,7 +128,7 @@ def tile_waveletgatednet_w_kernel(tc, x, W_words, W_scales, b, threshold, out):
 
         def stage_d(dh):
             x3 = fx.tile([P, 1024], BF16, name="x3")
-            nc.vector.tensor_copy(out=x3[:], in_=ps2s[dh][:].rearrange("p j e -> p (j e)"))
+            nc.scalar.copy(out=x3[:], in_=ps2s[dh][:].rearrange("p j e -> p (j e)"))
             x3s[dh] = x3
 
         def stage_e(dh):
@@ -167,7 +153,7 @@ def tile_waveletgatednet_w_kernel(tc, x, W_words, W_scales, b, threshold, out):
 
         def stage_h(dh):
             for hl in range(2):
-                ps4 = psz.tile([P, 4, P], F32, tag="z", name="ps4")
+                ps4 = psf.tile([P, 4, P], F32, tag="f", name="ps4")
                 for jl in range(4):
                     e0 = (4 * hl + jl) * P
                     nc.tensor.matmul(ps4[:, jl, :], lhsT=x3s[dh][:, e0 : e0 + P], rhs=g8[:], start=True, stop=True)
@@ -176,8 +162,8 @@ def tile_waveletgatednet_w_kernel(tc, x, W_words, W_scales, b, threshold, out):
         def stage_i(dh):
             for hl in range(2):
                 nc.scalar.copy(
-                    out=ut[:, 2 * dh + hl, :].rearrange("p (a j n) -> p a j n", j=4, n=4),
-                    in_=ps4s[(dh, hl)][:].rearrange("p j (a n) -> p a j n", n=4),
+                    out=ut[:, 2 * dh + hl, :].rearrange("p (c j n) -> p c j n", j=4, n=8),
+                    in_=ps4s[(dh, hl)][:].rearrange("p j (c n) -> p c j n", n=8),
                 )
 
         for s in range(7):
@@ -204,43 +190,36 @@ def tile_waveletgatednet_w_kernel(tc, x, W_words, W_scales, b, threshold, out):
         gates = {}
         gts = {}
         sqs = {}
-        y2s = {}
-        ngs = {}
+        y3s = {}
         pos = {}
         ots = {}
 
         def mx(hc):
             zs = []
-            if hc < 7:
-                zb = psf.tile([P, 4, P], F32, tag="f", name="zb")
+            for jl in range(4):
+                zt = psz.tile([P, P], F32, tag="z", name="zt")
+                zs.append(zt)
+            for g in range(8):
                 for jl in range(4):
-                    zs.append(zb[:, jl, :])
-                order = [(g, jl) for jl in range(4) for g in range(8)]
-            else:
-                for jl in range(4):
-                    zt = psz.tile([P, P], F32, tag="z", name="zt")
-                    zs.append(zt[:])
-                order = [(g, jl) for g in range(8) for jl in range(4)]
-            for g, jl in order:
-                n0 = 512 * hc + P * jl
-                nc.tensor.matmul_mx(
-                    out=zs[jl],
-                    lhsT=wts[hc][:, g, P * jl : P * jl + P].bitcast(FP8X4),
-                    lhsT_scale=planes[4 * (g % 4) : P, g // 4, n0 : n0 + P],
-                    rhs=cw[:, g, :].bitcast(FP8X4),
-                    rhs_scale=cs[:, g, :],
-                    start=(g == 0),
-                    stop=(g == 7),
-                )
+                    n0 = 512 * hc + P * jl
+                    nc.tensor.matmul_mx(
+                        out=zs[jl][:],
+                        lhsT=ww[:, g, n0 : n0 + P].bitcast(FP8X4),
+                        lhsT_scale=planes[4 * (g % 4) : P, g // 4, n0 : n0 + P],
+                        rhs=cw[:, g, :].bitcast(FP8X4),
+                        rhs_scale=cs[:, g, :],
+                        start=(g == 0),
+                        stop=(g == 7),
+                    )
             zss[hc] = zs
 
         def sig(hc):
-            gate = ep.tile([P, 32, 4, 4], F32, name="gate")
+            gate = ep.tile([P, 16, 4, 8], F32, name="gate")
             for jl in range(4):
                 eb = 4 * hc + jl
                 nc.scalar.activation(
                     out=gate[:, :, jl, :],
-                    in_=zss[hc][jl].rearrange("p (a n) -> p a n", n=4),
+                    in_=zss[hc][jl][:].rearrange("p (c n) -> p c n", n=8),
                     func=ACT.Sigmoid,
                     bias=bt[:, eb : eb + 1],
                     scale=1.0,
@@ -251,14 +230,14 @@ def tile_waveletgatednet_w_kernel(tc, x, W_words, W_scales, b, threshold, out):
             return ap4[:, :, 2 * a : 2 * a + 2, :].rearrange("p c j n -> p c (j n)")
 
         def prod(hc):
-            gt = ep.tile([P, 32, 4, 4], F32, name="gt")
-            utv = ut[:, hc, :].rearrange("p (a j n) -> p a j n", j=4, n=4)
+            gt = ep.tile([P, 16, 4, 8], F32, name="gt")
+            utv = ut[:, hc, :].rearrange("p (c j n) -> p c j n", j=4, n=8)
             for a in range(2):
                 nc.vector.tensor_tensor(out=half(gt[:], a), in0=half(gates[hc][:], a), in1=half(utv, a), op=ALU.mult)
             gts[hc] = gt
 
         def square(hc):
-            sq = ep.tile([P, 32, 4, 4], F32, name="sq")
+            sq = ep.tile([P, 16, 4, 8], F32, name="sq")
             for a in range(2):
                 nc.scalar.activation(out=half(sq[:], a), in_=half(gts[hc][:], a), func=ACT.Square)
             sqs[hc] = sq
@@ -269,53 +248,49 @@ def tile_waveletgatednet_w_kernel(tc, x, W_words, W_scales, b, threshold, out):
                 nc.vector.scalar_tensor_tensor(
                     out=half(sq[:], a), in0=half(sq[:], a), scalar=tsq[:, 0:1], in1=half(gts[hc][:], a), op0=ALU.is_ge, op1=ALU.mult
                 )
-            sl = sq[:].rearrange("p a j (r two) -> p (a j r) two", two=2)
+            sl = sq[:].rearrange("p c j (r two) -> p (c j r) two", two=2)
             y1 = ep.tile([P, 2, 128, 2], F32, name="y1")
             nc.vector.tensor_tensor(out=y1[:, 0].rearrange("p s two -> p (s two)"), in0=sl[:, :, 0], in1=sl[:, :, 1], op=ALU.add)
             nc.vector.tensor_tensor(out=y1[:, 1].rearrange("p s two -> p (s two)"), in0=sl[:, :, 0], in1=sl[:, :, 1], op=ALU.subtract)
+            y2 = ep.tile([P, 2, 2, 64, 2], F32, name="y2")
+            nc.vector.tensor_tensor(out=y2[:, 0].rearrange("p b s two -> p b (s two)"), in0=y1[:, :, :, 0], in1=y1[:, :, :, 1], op=ALU.add)
+            nc.vector.tensor_tensor(out=y2[:, 1].rearrange("p b s two -> p b (s two)"), in0=y1[:, :, :, 0], in1=y1[:, :, :, 1], op=ALU.subtract)
+            y2v = y2[:].rearrange("p a b (c j) two -> p (a b) c j two", j=4)
             dh = hc // 2
             hl = hc % 2
             if hl == 0:
-                y2n = ep.tile([P, 2, 2, 32, 2, 4], F32, name="y2")
-                y2s[dh] = y2n
-            y2 = y2s[dh]
-            y1v = y1[:].rearrange("p b (a j) two -> p b a j two", j=4)
-            nc.vector.tensor_tensor(out=y2[:, 0, :, :, hl, :], in0=y1v[:, :, :, :, 0], in1=y1v[:, :, :, :, 1], op=ALU.add)
-            nc.vector.tensor_tensor(out=y2[:, 1, :, :, hl, :], in0=y1v[:, :, :, :, 0], in1=y1v[:, :, :, :, 1], op=ALU.subtract)
-
-        def planes_of(dh):
-            return y2s[dh][:].rearrange("p x b (v c) h j -> p (x b) v (c h j)", v=2)
-
-        def neg(dh):
-            ng = ep.tile([P, 4, P], F32, name="ng")
-            nc.scalar.activation(out=ng[:], in_=planes_of(dh)[:, :, 1, :], func=ACT.Copy, scale=-1.0)
-            ngs[dh] = ng
+                y3n = ep.tile([P, 2, 4, 16, 2, 4], F32, name="y3")
+                y3s[dh] = y3n
+            y3 = y3s[dh]
+            nc.vector.tensor_tensor(out=y3[:, 0, :, :, hl, :], in0=y2v[:, :, :, :, 0], in1=y2v[:, :, :, :, 1], op=ALU.add)
+            nc.vector.tensor_tensor(out=y3[:, 1, :, :, hl, :], in0=y2v[:, :, :, :, 0], in1=y2v[:, :, :, :, 1], op=ALU.subtract)
 
         def back(dh):
-            yv = planes_of(dh)
-            for i2 in range(2):
+            y3p = y3s[dh][:].rearrange("p a b c h j -> p (a b) (c h j)")
+            for h in range(2):
                 po = pso.tile([P, 4, P], F32, tag="o", name="po")
                 for il in range(4):
-                    last = yv[:, il, 1, :] if i2 == 0 else ngs[dh][:, il, :]
-                    nc.tensor.matmul(po[:, il, :], lhsT=xpl[:, dh, 4 * i2 + il, :], rhs=ident_f[:], is_transpose=True, start=True, stop=False)
-                    nc.tensor.matmul(po[:, il, :], lhsT=yv[:, il, 0, :], rhs=ident_f[:], is_transpose=True, start=False, stop=False)
-                    nc.tensor.matmul(po[:, il, :], lhsT=last, rhs=ident_f[:], is_transpose=True, start=False, stop=True)
-                pos[(dh, i2)] = po
+                    nc.tensor.transpose(po[:, il, :], y3p[:, 4 * h + il, :], ident_f[:])
+                pos[(dh, h)] = po
 
         def fin(dh):
             ot = fx.tile([P, P, 8], F32, name="ot")
-            for i2 in range(2):
-                nc.scalar.copy(out=ot[:, :, 4 * i2 : 4 * i2 + 4], in_=pos[(dh, i2)][:].rearrange("p i e -> p e i"))
+            xr = xt[:, dh, :].rearrange("p (e i) -> p e i", i=8)
+            for h in range(2):
+                nc.vector.tensor_tensor(
+                    out=ot[:, :, 4 * h : 4 * h + 4],
+                    in0=pos[(dh, h)][:].rearrange("p i e -> p e i"),
+                    in1=xr[:, :, 4 * h : 4 * h + 4],
+                    op=ALU.add,
+                )
             ots[dh] = ot
 
         for hc in range(8):
             mx(hc)
-            if hc < 2:
-                load_w(hc + 6)
-            if hc in (0, 2, 4):
-                stage_h(hc // 2 + 1)
             if hc % 2 == 0 and hc >= 2:
                 back(hc // 2 - 1)
+            if hc in (0, 2, 4):
+                stage_h(hc // 2 + 1)
             sig(hc)
             prod(hc)
             square(hc)
@@ -324,8 +299,6 @@ def tile_waveletgatednet_w_kernel(tc, x, W_words, W_scales, b, threshold, out):
             if hc % 2 == 0 and hc >= 2:
                 fin(hc // 2 - 1)
             select_and_levels(hc)
-            if hc % 2 == 1:
-                neg(hc // 2)
         back(3)
         fin(3)
         for dh in range(4):

@@ -67,8 +67,13 @@ def tile_waveletgatednet_w_kernel(tc, x, W_words, W_scales, b, threshold, out):
                     out=ww[:, 2 * gp : 2 * gp + 2, cols].bitcast(I32),
                     in_=w32[2 * gp : 2 * gp + 2, :, cols].rearrange("g p n -> p g n"),
                 )
-        for g in range(8):
-            nc.sync.dma_start(out=ww[:, g, 3584:4096].bitcast(I32), in_=w32[g, :, 3584:4096])
+        for a in range(2):
+            cols = slice(3584 + 256 * a, 3840 + 256 * a)
+            for gp in range(4):
+                nc.sync.dma_start(
+                    out=ww[:, 2 * gp : 2 * gp + 2, cols].bitcast(I32),
+                    in_=w32[2 * gp : 2 * gp + 2, :, cols].rearrange("g p n -> p g n"),
+                )
 
         row_i = const.tile([P, P], I32)
         nc.gpsimd.iota(row_i[:], pattern=[[0, P]], base=0, channel_multiplier=1)
@@ -194,13 +199,13 @@ def tile_waveletgatednet_w_kernel(tc, x, W_words, W_scales, b, threshold, out):
         pos = {}
         ots = {}
 
-        def mx(hc):
-            zs = []
-            for jl in range(4):
+        def mx(hc, jls):
+            zs = zss.get(hc, {})
+            for jl in jls:
                 zt = psz.tile([P, P], F32, tag="z", name="zt")
-                zs.append(zt)
+                zs[jl] = zt
             for g in range(8):
-                for jl in range(4):
+                for jl in jls:
                     n0 = 512 * hc + P * jl
                     nc.tensor.matmul_mx(
                         out=zs[jl][:],
@@ -213,9 +218,12 @@ def tile_waveletgatednet_w_kernel(tc, x, W_words, W_scales, b, threshold, out):
                     )
             zss[hc] = zs
 
-        def sig(hc):
-            gate = ep.tile([P, 16, 4, 8], F32, name="gate")
-            for jl in range(4):
+        def sig(hc, jls):
+            if hc not in gates:
+                gnew = ep.tile([P, 16, 4, 8], F32, name="gate")
+                gates[hc] = gnew
+            gate = gates[hc]
+            for jl in jls:
                 eb = 4 * hc + jl
                 nc.scalar.activation(
                     out=gate[:, :, jl, :],
@@ -224,46 +232,61 @@ def tile_waveletgatednet_w_kernel(tc, x, W_words, W_scales, b, threshold, out):
                     bias=bt[:, eb : eb + 1],
                     scale=1.0,
                 )
-            gates[hc] = gate
 
         def half(ap4, a):
             return ap4[:, :, 2 * a : 2 * a + 2, :].rearrange("p c j n -> p c (j n)")
 
-        def prod(hc):
-            gt = ep.tile([P, 16, 4, 8], F32, name="gt")
+        def prod(hc, a):
+            if hc not in gts:
+                gtn = ep.tile([P, 16, 4, 8], F32, name="gt")
+                gts[hc] = gtn
             utv = ut[:, hc, :].rearrange("p (c j n) -> p c j n", j=4, n=8)
-            for a in range(2):
-                nc.vector.tensor_tensor(out=half(gt[:], a), in0=half(gates[hc][:], a), in1=half(utv, a), op=ALU.mult)
-            gts[hc] = gt
+            nc.vector.tensor_tensor(out=half(gts[hc][:], a), in0=half(gates[hc][:], a), in1=half(utv, a), op=ALU.mult)
 
-        def square(hc):
-            sq = ep.tile([P, 16, 4, 8], F32, name="sq")
-            for a in range(2):
-                nc.scalar.activation(out=half(sq[:], a), in_=half(gts[hc][:], a), func=ACT.Square)
-            sqs[hc] = sq
+        def square(hc, a):
+            if hc not in sqs:
+                sqn = ep.tile([P, 16, 4, 8], F32, name="sq")
+                sqs[hc] = sqn
+            nc.scalar.activation(out=half(sqs[hc][:], a), in_=half(gts[hc][:], a), func=ACT.Square)
 
-        def select_and_levels(hc):
+        def select(hc, a):
             sq = sqs[hc]
-            for a in range(2):
-                nc.vector.scalar_tensor_tensor(
-                    out=half(sq[:], a), in0=half(sq[:], a), scalar=tsq[:, 0:1], in1=half(gts[hc][:], a), op0=ALU.is_ge, op1=ALU.mult
+            nc.vector.scalar_tensor_tensor(
+                out=half(sq[:], a), in0=half(sq[:], a), scalar=tsq[:, 0:1], in1=half(gts[hc][:], a), op0=ALU.is_ge, op1=ALU.mult
+            )
+
+        y1s = {}
+        y2s = {}
+
+        def level1(hc, j0, j1):
+            if hc not in y1s:
+                y1n = ep.tile([P, 2, 16, 4, 4], F32, name="y1")
+                y1s[hc] = y1n
+            src = sqs[hc][:, :, j0:j1, :].rearrange("p c j (r two) -> p c (j r) two", two=2)
+            for bb, op in ((0, ALU.add), (1, ALU.subtract)):
+                nc.vector.tensor_tensor(
+                    out=y1s[hc][:, bb, :, j0:j1, :].rearrange("p c j r -> p c (j r)"), in0=src[:, :, :, 0], in1=src[:, :, :, 1], op=op
                 )
-            sl = sq[:].rearrange("p c j (r two) -> p (c j r) two", two=2)
-            y1 = ep.tile([P, 2, 128, 2], F32, name="y1")
-            nc.vector.tensor_tensor(out=y1[:, 0].rearrange("p s two -> p (s two)"), in0=sl[:, :, 0], in1=sl[:, :, 1], op=ALU.add)
-            nc.vector.tensor_tensor(out=y1[:, 1].rearrange("p s two -> p (s two)"), in0=sl[:, :, 0], in1=sl[:, :, 1], op=ALU.subtract)
-            y2 = ep.tile([P, 2, 2, 64, 2], F32, name="y2")
-            nc.vector.tensor_tensor(out=y2[:, 0].rearrange("p b s two -> p b (s two)"), in0=y1[:, :, :, 0], in1=y1[:, :, :, 1], op=ALU.add)
-            nc.vector.tensor_tensor(out=y2[:, 1].rearrange("p b s two -> p b (s two)"), in0=y1[:, :, :, 0], in1=y1[:, :, :, 1], op=ALU.subtract)
-            y2v = y2[:].rearrange("p a b (c j) two -> p (a b) c j two", j=4)
+
+        def level2(hc, j0, j1):
+            if hc not in y2s:
+                y2n = ep.tile([P, 2, 2, 16, 4, 2], F32, name="y2")
+                y2s[hc] = y2n
+            src = y1s[hc][:, :, :, j0:j1, :].rearrange("p b c j (r two) -> p b c (j r) two", two=2)
+            for bb, op in ((0, ALU.add), (1, ALU.subtract)):
+                nc.vector.tensor_tensor(
+                    out=y2s[hc][:, bb, :, :, j0:j1, :].rearrange("p b c j r -> p b c (j r)"), in0=src[:, :, :, :, 0], in1=src[:, :, :, :, 1], op=op
+                )
+
+        def level3(hc):
             dh = hc // 2
             hl = hc % 2
             if hl == 0:
                 y3n = ep.tile([P, 2, 4, 16, 2, 4], F32, name="y3")
                 y3s[dh] = y3n
-            y3 = y3s[dh]
-            nc.vector.tensor_tensor(out=y3[:, 0, :, :, hl, :], in0=y2v[:, :, :, :, 0], in1=y2v[:, :, :, :, 1], op=ALU.add)
-            nc.vector.tensor_tensor(out=y3[:, 1, :, :, hl, :], in0=y2v[:, :, :, :, 0], in1=y2v[:, :, :, :, 1], op=ALU.subtract)
+            src = y2s[hc][:].rearrange("p x b c j two -> p (x b) c j two")
+            for bb, op in ((0, ALU.add), (1, ALU.subtract)):
+                nc.vector.tensor_tensor(out=y3s[dh][:, bb, :, :, hl, :], in0=src[:, :, :, :, 0], in1=src[:, :, :, :, 1], op=op)
 
         def back(dh):
             y3p = y3s[dh][:].rearrange("p a b c h j -> p (a b) (c h j)")
@@ -285,20 +308,35 @@ def tile_waveletgatednet_w_kernel(tc, x, W_words, W_scales, b, threshold, out):
                 )
             ots[dh] = ot
 
-        for hc in range(8):
-            mx(hc)
+        for hc in range(7):
+            mx(hc, (0, 1, 2, 3))
             if hc % 2 == 0 and hc >= 2:
                 back(hc // 2 - 1)
             if hc in (0, 2, 4):
                 stage_h(hc // 2 + 1)
-            sig(hc)
-            prod(hc)
-            square(hc)
+            sig(hc, (0, 1, 2, 3))
+            prod(hc, 0)
+            prod(hc, 1)
+            square(hc, 0)
+            square(hc, 1)
             if hc in (0, 2, 4):
                 stage_i(hc // 2 + 1)
             if hc % 2 == 0 and hc >= 2:
                 fin(hc // 2 - 1)
-            select_and_levels(hc)
+            select(hc, 0)
+            select(hc, 1)
+            level1(hc, 0, 4)
+            level2(hc, 0, 4)
+            level3(hc)
+        for a in range(2):
+            mx(7, (2 * a, 2 * a + 1))
+            sig(7, (2 * a, 2 * a + 1))
+            prod(7, a)
+            square(7, a)
+            select(7, a)
+            level1(7, 2 * a, 2 * a + 2)
+            level2(7, 2 * a, 2 * a + 2)
+        level3(7)
         back(3)
         fin(3)
         for dh in range(4):

@@ -26,6 +26,8 @@ def tile_waveletgatednet_w_kernel(tc, x, W_words, W_scales, b, threshold, out):
         fw = ctx.enter_context(tc.tile_pool(name="fw", bufs=2))
         fx = ctx.enter_context(tc.tile_pool(name="fx", bufs=4))
         ep = ctx.enter_context(tc.tile_pool(name="ep", bufs=2))
+        e1 = ctx.enter_context(tc.tile_pool(name="e1", bufs=1))
+        wp = ctx.enter_context(tc.tile_pool(name="wp", bufs=3))
         psz = ctx.enter_context(tc.psum_pool(name="psz", bufs=4))
         pso = ctx.enter_context(tc.psum_pool(name="pso", bufs=2))
         psf = ctx.enter_context(tc.psum_pool(name="psf", bufs=2))
@@ -33,12 +35,11 @@ def tile_waveletgatednet_w_kernel(tc, x, W_words, W_scales, b, threshold, out):
 
         planes = keep.tile([P, 2, D], U8, align_bytes=64)
         xt = keep.tile([P, 4, 1024], BF16)
-        ww = keep.tile([P, 8, D], U32, align_bytes=64)
         cw = keep.tile([P, 8, P], U32, align_bytes=64)
         cs = keep.tile([P, 8, P], U8, align_bytes=64)
-        ut = keep.tile([P, 8, 512], F32)
+        ut = keep.tile([P, 4, 16, 8, 8], F32)
 
-        nc.vector.memset(planes[:].rearrange("p a n -> p (a n)").bitcast(I32), 0)
+        nc.vector.memset(planes[:, 0, :].bitcast(I32), 0)
         btile = const.tile([P, P], BF16)
         nc.vector.memset(btile[:], 0.0)
         warm = const.tile([P, 1], F32)
@@ -53,6 +54,15 @@ def tile_waveletgatednet_w_kernel(tc, x, W_words, W_scales, b, threshold, out):
         nc.scalar.dma_start(out=thr_b[:], in_=threshold.partition_broadcast(P))
         warm2 = const.tile([P, 1], F32)
         nc.scalar.activation(out=warm2[:], in_=warm[:], func=ACT.Sigmoid)
+        row_i = const.tile([P, P], I32)
+        nc.gpsimd.iota(row_i[:], pattern=[[0, P]], base=0, channel_multiplier=1)
+        col_i = const.tile([P, P], I32)
+        nc.gpsimd.iota(col_i[:], pattern=[[1, P]], base=0, channel_multiplier=0)
+        ident_f = const.tile([P, P], F32)
+        make_identity(nc, ident_f[:])
+        nc.gpsimd.memset(planes[:, 1, :].bitcast(F32), 0.0)
+        ident_b = const.tile([P, P], BF16)
+        make_identity(nc, ident_b[:])
         for a in range(2):
             for q in (0, 2, 1, 3):
                 nc.sync.dma_start(
@@ -60,29 +70,26 @@ def tile_waveletgatednet_w_kernel(tc, x, W_words, W_scales, b, threshold, out):
                     in_=W_scales[4 * a : 4 * a + 4, 4 * q : 4 * q + 4, :].bitcast(I32),
                 )
         w32 = W_words.rearrange("g p n t -> g p (n t)").bitcast(I32)
-        for hc in range(7):
-            cols = slice(512 * hc, 512 * (hc + 1))
-            for gp in range(4):
-                nc.sync.dma_start(
-                    out=ww[:, 2 * gp : 2 * gp + 2, cols].bitcast(I32),
-                    in_=w32[2 * gp : 2 * gp + 2, :, cols].rearrange("g p n -> p g n"),
-                )
-        for a in range(2):
-            cols = slice(3584 + 256 * a, 3840 + 256 * a)
-            for gp in range(4):
-                nc.sync.dma_start(
-                    out=ww[:, 2 * gp : 2 * gp + 2, cols].bitcast(I32),
-                    in_=w32[2 * gp : 2 * gp + 2, :, cols].rearrange("g p n -> p g n"),
-                )
+        wts = {}
 
-        row_i = const.tile([P, P], I32)
-        nc.gpsimd.iota(row_i[:], pattern=[[0, P]], base=0, channel_multiplier=1)
-        col_i = const.tile([P, P], I32)
-        nc.gpsimd.iota(col_i[:], pattern=[[1, P]], base=0, channel_multiplier=0)
-        ident_f = const.tile([P, P], F32)
-        make_identity(nc, ident_f[:])
-        ident_b = const.tile([P, P], BF16)
-        make_identity(nc, ident_b[:])
+        def load_w(dh):
+            wt = wp.tile([P, 8, 1024], U32, align_bytes=64, name="wt")
+            wts[dh] = wt
+            for hl in range(2):
+                c0 = 1024 * dh + 512 * hl
+                if dh < 3 or hl == 0:
+                    for gp in range(4):
+                        nc.sync.dma_start(
+                            out=wt[:, 2 * gp : 2 * gp + 2, 512 * hl : 512 * hl + 512].bitcast(I32),
+                            in_=w32[2 * gp : 2 * gp + 2, :, c0 : c0 + 512].rearrange("g p n -> p g n"),
+                        )
+                else:
+                    for g in range(8):
+                        nc.sync.dma_start(out=wt[:, g, 512:1024].bitcast(I32), in_=w32[g, :, c0 : c0 + 512])
+
+        for dh in range(3):
+            load_w(dh)
+
         both = const.tile([P, P], I32)
         nc.vector.tensor_tensor(out=both[:], in0=row_i[:], in1=col_i[:], op=ALU.bitwise_and)
         sh1 = const.tile([P, P], I32)
@@ -121,19 +128,19 @@ def tile_waveletgatednet_w_kernel(tc, x, W_words, W_scales, b, threshold, out):
 
         def stage_b(dh):
             rw = fw.tile([P, 8, 16, 4], F32, name="rw")
-            nc.vector.tensor_copy(out=rw[:], in_=ps1s[dh][:].rearrange("p m (c j) -> p j c m", j=8))
+            nc.scalar.copy(out=rw[:], in_=ps1s[dh][:].rearrange("p m (c j) -> p j c m", j=8))
             rws[dh] = rw
 
         def stage_c(dh):
             rb = rws[dh][:].rearrange("p j c m -> p j (c m)").bitcast(BF16)
-            ps2 = psz.tile([P, 8, P], BF16, tag="z", name="ps2")
+            ps2 = psf.tile([P, 8, P], BF16, tag="f", name="ps2")
             for jj in range(8):
                 nc.tensor.transpose(ps2[:, jj, :], rb[:, jj, :], ident_b[:])
             ps2s[dh] = ps2
 
         def stage_d(dh):
             x3 = fx.tile([P, 1024], BF16, name="x3")
-            nc.scalar.copy(out=x3[:], in_=ps2s[dh][:].rearrange("p j e -> p (j e)"))
+            nc.vector.tensor_copy(out=x3[:], in_=ps2s[dh][:].rearrange("p j e -> p (j e)"))
             x3s[dh] = x3
 
         def stage_e(dh):
@@ -167,9 +174,129 @@ def tile_waveletgatednet_w_kernel(tc, x, W_words, W_scales, b, threshold, out):
         def stage_i(dh):
             for hl in range(2):
                 nc.scalar.copy(
-                    out=ut[:, 2 * dh + hl, :].rearrange("p (c j n) -> p c j n", j=4, n=8),
+                    out=ut[:, dh, :, 4 * hl : 4 * hl + 4, :],
                     in_=ps4s[(dh, hl)][:].rearrange("p j (c n) -> p c j n", n=8),
                 )
+
+
+        zss = {}
+        gates = {}
+        gts = {}
+        sqs = {}
+        y1s = {}
+        y2s = {}
+        y3s = {}
+        pos = {}
+        ots = {}
+        ADD_SUB = ((0, ALU.add), (1, ALU.subtract))
+
+        def mx(hc, g0=0, g1=8):
+            if g0 == 0:
+                zn = []
+                for jl in range(4):
+                    zt = psz.tile([P, P], F32, tag="z", name="zt")
+                    zn.append(zt[:])
+                zss[hc] = zn
+            zs = zss[hc]
+            for g, jl in [(g, jl) for g in range(g0, g1) for jl in range(4)]:
+                n0 = 512 * hc + P * jl
+                w0 = 512 * (hc % 2) + P * jl
+                nc.tensor.matmul_mx(
+                    out=zs[jl],
+                    lhsT=wts[hc // 2][:, g, w0 : w0 + P].bitcast(FP8X4),
+                    lhsT_scale=planes[4 * (g % 4) : P, g // 4, n0 : n0 + P],
+                    rhs=cw[:, g, :].bitcast(FP8X4),
+                    rhs_scale=cs[:, g, :],
+                    start=(g == 0),
+                    stop=(g == 7),
+                )
+
+        def part(tile4, hc):
+            hl = hc % 2
+            return tile4[:, :, 4 * hl : 4 * hl + 4, :].rearrange("p c j n -> p c (j n)")
+
+        def sig(hc):
+            dh = hc // 2
+            if hc % 2 == 0:
+                gnew = ep.tile([P, 16, 8, 8], F32, name="gate")
+                gates[dh] = gnew
+            for jl in range(4):
+                eb = 4 * hc + jl
+                nc.scalar.activation(
+                    out=gates[dh][:, :, 4 * (hc % 2) + jl, :],
+                    in_=zss[hc][jl].rearrange("p (c n) -> p c n", n=8),
+                    func=ACT.Sigmoid,
+                    bias=bt[:, eb : eb + 1],
+                    scale=1.0,
+                )
+
+        def prod(hc):
+            dh = hc // 2
+            if hc % 2 == 0:
+                gtn = ep.tile([P, 16, 8, 8], F32, name="gt")
+                gts[dh] = gtn
+            nc.vector.tensor_tensor(out=part(gts[dh][:], hc), in0=part(gates[dh][:], hc), in1=part(ut[:, dh], hc), op=ALU.mult)
+
+        def square(hc):
+            dh = hc // 2
+            if hc % 2 == 0:
+                sqn = ep.tile([P, 16, 8, 8], F32, name="sq")
+                sqs[dh] = sqn
+            nc.scalar.activation(out=part(sqs[dh][:], hc), in_=part(gts[dh][:], hc), func=ACT.Square)
+
+        def select(hc):
+            dh = hc // 2
+            nc.vector.scalar_tensor_tensor(
+                out=part(sqs[dh][:], hc), in0=part(sqs[dh][:], hc), scalar=tsq[:, 0:1], in1=part(gts[dh][:], hc), op0=ALU.is_ge, op1=ALU.mult
+            )
+
+        def level1(dh, j0, j1):
+            if dh not in y1s:
+                y1n = e1.tile([P, 2, 16, 8, 4], F32, name="y1")
+                y1s[dh] = y1n
+            src = sqs[dh][:, :, j0:j1, :].rearrange("p c j (r two) -> p c (j r) two", two=2)
+            for bb, op in ADD_SUB:
+                nc.vector.tensor_tensor(
+                    out=y1s[dh][:, bb, :, j0:j1, :].rearrange("p c j r -> p c (j r)"), in0=src[:, :, :, 0], in1=src[:, :, :, 1], op=op
+                )
+
+        def level2(dh, j0, j1):
+            if dh not in y2s:
+                y2n = e1.tile([P, 2, 2, 16, 8, 2], F32, name="y2")
+                y2s[dh] = y2n
+            src = y1s[dh][:, :, :, j0:j1, :].rearrange("p b c j (r two) -> p b c (j r) two", two=2)
+            for bb, op in ADD_SUB:
+                nc.vector.tensor_tensor(
+                    out=y2s[dh][:, bb, :, :, j0:j1, :].rearrange("p b c j r -> p b c (j r)"), in0=src[:, :, :, :, 0], in1=src[:, :, :, :, 1], op=op
+                )
+
+        def level3(dh, j0, j1):
+            if dh not in y3s:
+                y3n = ep.tile([P, 2, 4, 16, 8], F32, name="y3")
+                y3s[dh] = y3n
+            src = y2s[dh][:, :, :, :, j0:j1, :].rearrange("p x b c j two -> p (x b) c j two")
+            for bb, op in ADD_SUB:
+                nc.vector.tensor_tensor(out=y3s[dh][:, bb, :, :, j0:j1], in0=src[:, :, :, :, 0], in1=src[:, :, :, :, 1], op=op)
+
+        def back(dh):
+            y3p = y3s[dh][:].rearrange("p h i c j -> p h i (c j)")
+            for h in range(2):
+                po = pso.tile([P, 4, P], F32, tag="o", name="po")
+                for il in range(4):
+                    nc.tensor.transpose(po[:, il, :], y3p[:, h, il, :], ident_f[:])
+                pos[(dh, h)] = po
+
+        def fin(dh, h):
+            if h == 0:
+                otn = fx.tile([P, P, 8], F32, name="ot")
+                ots[dh] = otn
+            xr = xt[:, dh, :].rearrange("p (e i) -> p e i", i=8)
+            nc.vector.tensor_tensor(
+                out=ots[dh][:, :, 4 * h : 4 * h + 4],
+                in0=pos[(dh, h)][:].rearrange("p i e -> p e i"),
+                in1=xr[:, :, 4 * h : 4 * h + 4],
+                op=ALU.add,
+            )
 
         for s in range(7):
             if s < 4:
@@ -184,160 +311,60 @@ def tile_waveletgatednet_w_kernel(tc, x, W_words, W_scales, b, threshold, out):
                 stage_e(s - 2)
                 stage_f(s - 2)
             if s == 3:
-                psb = psz.tile([P, P], BF16, tag="z", name="psb")
+                psb = pso.tile([P, P], BF16, tag="o", name="psb")
                 nc.tensor.transpose(psb[:], btile[:], ident_b[:])
                 nc.vector.tensor_copy(out=bt[:], in_=psb[:, 0:32])
                 nc.vector.scalar_tensor_tensor(out=tsq[:], in0=thr_b[:], scalar=0.125, in1=thr_b[:], op0=ALU.mult, op1=ALU.mult)
+            if s >= 4:
+                mx(0, 2 * (s - 4), 2 * (s - 4) + 2)
         stage_h(0)
         stage_i(0)
-
-        zss = {}
-        gates = {}
-        gts = {}
-        sqs = {}
-        y3s = {}
-        pos = {}
-        ots = {}
-
-        def mx(hc, jls):
-            zs = zss.get(hc, {})
-            for jl in jls:
-                zt = psz.tile([P, P], F32, tag="z", name="zt")
-                zs[jl] = zt
-            for g in range(8):
-                for jl in jls:
-                    n0 = 512 * hc + P * jl
-                    nc.tensor.matmul_mx(
-                        out=zs[jl][:],
-                        lhsT=ww[:, g, n0 : n0 + P].bitcast(FP8X4),
-                        lhsT_scale=planes[4 * (g % 4) : P, g // 4, n0 : n0 + P],
-                        rhs=cw[:, g, :].bitcast(FP8X4),
-                        rhs_scale=cs[:, g, :],
-                        start=(g == 0),
-                        stop=(g == 7),
-                    )
-            zss[hc] = zs
-
-        def sig(hc, jls):
-            if hc not in gates:
-                gnew = ep.tile([P, 16, 4, 8], F32, name="gate")
-                gates[hc] = gnew
-            gate = gates[hc]
-            for jl in jls:
-                eb = 4 * hc + jl
-                nc.scalar.activation(
-                    out=gate[:, :, jl, :],
-                    in_=zss[hc][jl][:].rearrange("p (c n) -> p c n", n=8),
-                    func=ACT.Sigmoid,
-                    bias=bt[:, eb : eb + 1],
-                    scale=1.0,
-                )
-
-        def half(ap4, a):
-            return ap4[:, :, 2 * a : 2 * a + 2, :].rearrange("p c j n -> p c (j n)")
-
-        def prod(hc, a):
-            if hc not in gts:
-                gtn = ep.tile([P, 16, 4, 8], F32, name="gt")
-                gts[hc] = gtn
-            utv = ut[:, hc, :].rearrange("p (c j n) -> p c j n", j=4, n=8)
-            nc.vector.tensor_tensor(out=half(gts[hc][:], a), in0=half(gates[hc][:], a), in1=half(utv, a), op=ALU.mult)
-
-        def square(hc, a):
-            if hc not in sqs:
-                sqn = ep.tile([P, 16, 4, 8], F32, name="sq")
-                sqs[hc] = sqn
-            nc.scalar.activation(out=half(sqs[hc][:], a), in_=half(gts[hc][:], a), func=ACT.Square)
-
-        def select(hc, a):
-            sq = sqs[hc]
-            nc.vector.scalar_tensor_tensor(
-                out=half(sq[:], a), in0=half(sq[:], a), scalar=tsq[:, 0:1], in1=half(gts[hc][:], a), op0=ALU.is_ge, op1=ALU.mult
-            )
-
-        y1s = {}
-        y2s = {}
-
-        def level1(hc, j0, j1):
-            if hc not in y1s:
-                y1n = ep.tile([P, 2, 16, 4, 4], F32, name="y1")
-                y1s[hc] = y1n
-            src = sqs[hc][:, :, j0:j1, :].rearrange("p c j (r two) -> p c (j r) two", two=2)
-            for bb, op in ((0, ALU.add), (1, ALU.subtract)):
-                nc.vector.tensor_tensor(
-                    out=y1s[hc][:, bb, :, j0:j1, :].rearrange("p c j r -> p c (j r)"), in0=src[:, :, :, 0], in1=src[:, :, :, 1], op=op
-                )
-
-        def level2(hc, j0, j1):
-            if hc not in y2s:
-                y2n = ep.tile([P, 2, 2, 16, 4, 2], F32, name="y2")
-                y2s[hc] = y2n
-            src = y1s[hc][:, :, :, j0:j1, :].rearrange("p b c j (r two) -> p b c (j r) two", two=2)
-            for bb, op in ((0, ALU.add), (1, ALU.subtract)):
-                nc.vector.tensor_tensor(
-                    out=y2s[hc][:, bb, :, :, j0:j1, :].rearrange("p b c j r -> p b c (j r)"), in0=src[:, :, :, :, 0], in1=src[:, :, :, :, 1], op=op
-                )
-
-        def level3(hc):
-            dh = hc // 2
-            hl = hc % 2
-            if hl == 0:
-                y3n = ep.tile([P, 2, 4, 16, 2, 4], F32, name="y3")
-                y3s[dh] = y3n
-            src = y2s[hc][:].rearrange("p x b c j two -> p (x b) c j two")
-            for bb, op in ((0, ALU.add), (1, ALU.subtract)):
-                nc.vector.tensor_tensor(out=y3s[dh][:, bb, :, :, hl, :], in0=src[:, :, :, :, 0], in1=src[:, :, :, :, 1], op=op)
-
-        def back(dh):
-            y3p = y3s[dh][:].rearrange("p a b c h j -> p (a b) (c h j)")
-            for h in range(2):
-                po = pso.tile([P, 4, P], F32, tag="o", name="po")
-                for il in range(4):
-                    nc.tensor.transpose(po[:, il, :], y3p[:, 4 * h + il, :], ident_f[:])
-                pos[(dh, h)] = po
-
-        def fin(dh):
-            ot = fx.tile([P, P, 8], F32, name="ot")
-            xr = xt[:, dh, :].rearrange("p (e i) -> p e i", i=8)
-            for h in range(2):
-                nc.vector.tensor_tensor(
-                    out=ot[:, :, 4 * h : 4 * h + 4],
-                    in0=pos[(dh, h)][:].rearrange("p i e -> p e i"),
-                    in1=xr[:, :, 4 * h : 4 * h + 4],
-                    op=ALU.add,
-                )
-            ots[dh] = ot
-
-        for hc in range(7):
-            mx(hc, (0, 1, 2, 3))
-            if hc % 2 == 0 and hc >= 2:
-                back(hc // 2 - 1)
-            if hc in (0, 2, 4):
-                stage_h(hc // 2 + 1)
-            sig(hc, (0, 1, 2, 3))
-            prod(hc, 0)
-            prod(hc, 1)
-            square(hc, 0)
-            square(hc, 1)
-            if hc in (0, 2, 4):
-                stage_i(hc // 2 + 1)
-            if hc % 2 == 0 and hc >= 2:
-                fin(hc // 2 - 1)
-            select(hc, 0)
-            select(hc, 1)
-            level1(hc, 0, 4)
-            level2(hc, 0, 4)
-            level3(hc)
-        for a in range(2):
-            mx(7, (2 * a, 2 * a + 1))
-            sig(7, (2 * a, 2 * a + 1))
-            prod(7, a)
-            square(7, a)
-            select(7, a)
-            level1(7, 2 * a, 2 * a + 2)
-            level2(7, 2 * a, 2 * a + 2)
-        level3(7)
+        mx(0, 6, 8)
+        sig(0)
+        prod(0)
+        square(0)
+        mx(1)
+        load_w(3)
+        stage_h(1)
+        sig(1)
+        stage_i(1)
+        select(0)
+        prod(1)
+        square(1)
+        level1(0, 0, 4)
+        level2(0, 0, 4)
+        mx(2)
+        sig(2)
+        select(1)
+        level3(0, 0, 4)
+        level1(0, 4, 8)
+        level2(0, 4, 8)
+        prod(2)
+        level3(0, 4, 8)
+        mx(3)
+        for dh in range(1, 4):
+            sig(2 * dh + 1)
+            square(2 * dh)
+            prod(2 * dh + 1)
+            square(2 * dh + 1)
+            back(dh - 1)
+            if dh < 3:
+                stage_h(dh + 1)
+                stage_i(dh + 1)
+                mx(2 * dh + 2)
+                sig(2 * dh + 2)
+                mx(2 * dh + 3)
+            select(2 * dh)
+            fin(dh - 1, 0)
+            select(2 * dh + 1)
+            fin(dh - 1, 1)
+            level1(dh, 0, 8)
+            level2(dh, 0, 8)
+            if dh < 3:
+                prod(2 * dh + 2)
+            level3(dh, 0, 8)
         back(3)
-        fin(3)
+        fin(3, 0)
+        fin(3, 1)
         for dh in range(4):
             nc.sync.dma_start(out=ov[:, :, dh, :], in_=ots[dh][:].rearrange("p e i -> p (e i)"))

@@ -38,6 +38,7 @@ def tile_waveletgatednet_w_kernel(tc, x, W_words, W_scales, b, threshold, out):
         cw = keep.tile([P, 8, P], U32, align_bytes=64)
         cs = keep.tile([P, 8, P], U8, align_bytes=64)
         ut = keep.tile([P, 4, 16, 8, 8], F32)
+        xpl = keep.tile([P, 8, P], F32)
 
         nc.vector.memset(planes[:, 0, :].bitcast(I32), 0)
         btile = const.tile([P, P], BF16)
@@ -127,9 +128,18 @@ def tile_waveletgatednet_w_kernel(tc, x, W_words, W_scales, b, threshold, out):
             ps1s[dh] = ps1
 
         def stage_b(dh):
-            rw = fw.tile([P, 8, 16, 4], F32, name="rw")
+            rw = fx.tile([P, 8, 16, 4], F32, name="rw")
             nc.scalar.copy(out=rw[:], in_=ps1s[dh][:].rearrange("p m (c j) -> p j c m", j=8))
             rws[dh] = rw
+            if dh == 2:
+                nc.gpsimd.tensor_scalar(
+                    out=xpl[:].rearrange("p i (c j) -> p i c j", j=8),
+                    in0=rw[:].rearrange("p j c m -> p j (c m)").bitcast(BF16).rearrange("p j (c i) -> p i c j", i=8),
+                    scalar1=1.0,
+                    scalar2=0.0,
+                    op0=ALU.mult,
+                    op1=ALU.add,
+                )
 
         def stage_c(dh):
             rb = rws[dh][:].rearrange("p j c m -> p j (c m)").bitcast(BF16)
@@ -283,13 +293,20 @@ def tile_waveletgatednet_w_kernel(tc, x, W_words, W_scales, b, threshold, out):
             for h in range(2):
                 po = pso.tile([P, 4, P], F32, tag="o", name="po")
                 for il in range(4):
-                    nc.tensor.transpose(po[:, il, :], y3p[:, h, il, :], ident_f[:])
+                    if dh == 2:
+                        nc.tensor.matmul(po[:, il, :], lhsT=xpl[:, 4 * h + il, :], rhs=ident_f[:], is_transpose=True, start=True, stop=False)
+                        nc.tensor.matmul(po[:, il, :], lhsT=y3p[:, h, il, :], rhs=ident_f[:], is_transpose=True, start=False, stop=True)
+                    else:
+                        nc.tensor.transpose(po[:, il, :], y3p[:, h, il, :], ident_f[:])
                 pos[(dh, h)] = po
 
         def fin(dh, h):
             if h == 0:
                 otn = fx.tile([P, P, 8], F32, name="ot")
                 ots[dh] = otn
+            if dh == 2:
+                nc.scalar.copy(out=ots[dh][:, :, 4 * h : 4 * h + 4], in_=pos[(dh, h)][:].rearrange("p i e -> p e i"))
+                return
             xr = xt[:, dh, :].rearrange("p (e i) -> p e i", i=8)
             nc.vector.tensor_tensor(
                 out=ots[dh][:, :, 4 * h : 4 * h + 4],

@@ -38,7 +38,6 @@ def tile_waveletgatednet_w_kernel(tc, x, W_words, W_scales, b, threshold, out):
         cw = keep.tile([P, 8, P], U32, align_bytes=64)
         cs = keep.tile([P, 8, P], U8, align_bytes=64)
         ut = keep.tile([P, 4, 16, 8, 8], F32)
-        xpl = keep.tile([P, 8, P], F32)
 
         nc.vector.memset(planes[:, 0, :].bitcast(I32), 0)
         btile = const.tile([P, P], BF16)
@@ -128,18 +127,9 @@ def tile_waveletgatednet_w_kernel(tc, x, W_words, W_scales, b, threshold, out):
             ps1s[dh] = ps1
 
         def stage_b(dh):
-            rw = fx.tile([P, 8, 16, 4], F32, name="rw")
+            rw = fw.tile([P, 8, 16, 4], F32, name="rw")
             nc.scalar.copy(out=rw[:], in_=ps1s[dh][:].rearrange("p m (c j) -> p j c m", j=8))
             rws[dh] = rw
-            if dh == 2:
-                nc.gpsimd.tensor_scalar(
-                    out=xpl[:].rearrange("p i (c j) -> p i c j", j=8),
-                    in0=rw[:].rearrange("p j c m -> p j (c m)").bitcast(BF16).rearrange("p j (c i) -> p i c j", i=8),
-                    scalar1=1.0,
-                    scalar2=0.0,
-                    op0=ALU.mult,
-                    op1=ALU.add,
-                )
 
         def stage_c(dh):
             rb = rws[dh][:].rearrange("p j c m -> p j (c m)").bitcast(BF16)
@@ -293,20 +283,13 @@ def tile_waveletgatednet_w_kernel(tc, x, W_words, W_scales, b, threshold, out):
             for h in range(2):
                 po = pso.tile([P, 4, P], F32, tag="o", name="po")
                 for il in range(4):
-                    if dh == 2:
-                        nc.tensor.matmul(po[:, il, :], lhsT=xpl[:, 4 * h + il, :], rhs=ident_f[:], is_transpose=True, start=True, stop=False)
-                        nc.tensor.matmul(po[:, il, :], lhsT=y3p[:, h, il, :], rhs=ident_f[:], is_transpose=True, start=False, stop=True)
-                    else:
-                        nc.tensor.transpose(po[:, il, :], y3p[:, h, il, :], ident_f[:])
+                    nc.tensor.transpose(po[:, il, :], y3p[:, h, il, :], ident_f[:])
                 pos[(dh, h)] = po
 
         def fin(dh, h):
             if h == 0:
                 otn = fx.tile([P, P, 8], F32, name="ot")
                 ots[dh] = otn
-            if dh == 2:
-                nc.scalar.copy(out=ots[dh][:, :, 4 * h : 4 * h + 4], in_=pos[(dh, h)][:].rearrange("p i e -> p e i"))
-                return
             xr = xt[:, dh, :].rearrange("p (e i) -> p e i", i=8)
             nc.vector.tensor_tensor(
                 out=ots[dh][:, :, 4 * h : 4 * h + 4],
@@ -337,49 +320,38 @@ def tile_waveletgatednet_w_kernel(tc, x, W_words, W_scales, b, threshold, out):
         stage_h(0)
         stage_i(0)
         mx(0, 6, 8)
-        sig(0)
-        prod(0)
-        square(0)
-        mx(1)
-        load_w(3)
-        stage_h(1)
-        sig(1)
-        stage_i(1)
-        select(0)
-        prod(1)
-        square(1)
-        level1(0, 0, 4)
-        level2(0, 0, 4)
-        mx(2)
-        sig(2)
-        select(1)
-        level3(0, 0, 4)
-        level1(0, 4, 8)
-        level2(0, 4, 8)
-        prod(2)
-        level3(0, 4, 8)
-        mx(3)
-        for dh in range(1, 4):
-            sig(2 * dh + 1)
-            square(2 * dh)
-            prod(2 * dh + 1)
-            square(2 * dh + 1)
-            back(dh - 1)
+        for dh in range(4):
+            even = 2 * dh
+            odd = even + 1
+            sig(even)
+            prod(even)
+            square(even)
+            mx(odd, 0, 4)
+            if dh > 0:
+                back(dh - 1)
+            mx(odd, 4, 8)
+            if dh == 0:
+                load_w(3)
             if dh < 3:
                 stage_h(dh + 1)
-                stage_i(dh + 1)
-                mx(2 * dh + 2)
-                sig(2 * dh + 2)
-                mx(2 * dh + 3)
-            select(2 * dh)
-            fin(dh - 1, 0)
-            select(2 * dh + 1)
-            fin(dh - 1, 1)
-            level1(dh, 0, 8)
-            level2(dh, 0, 8)
+            if dh > 0:
+                fin(dh - 1, 0)
+                fin(dh - 1, 1)
+            select(even)
+            level1(dh, 0, 4)
+            sig(odd)
+            prod(odd)
+            square(odd)
             if dh < 3:
-                prod(2 * dh + 2)
-            level3(dh, 0, 8)
+                stage_i(dh + 1)
+                mx(even + 2, 0, 4)
+                mx(even + 2, 4, 8)
+            level2(dh, 0, 4)
+            select(odd)
+            level3(dh, 0, 4)
+            level1(dh, 4, 8)
+            level2(dh, 4, 8)
+            level3(dh, 4, 8)
         back(3)
         fin(3, 0)
         fin(3, 1)

@@ -163,16 +163,16 @@ def tile_waveletgatednet_w_kernel(tc, x, W_words, W_scales, b, threshold, out):
                 in_=grps[dh][:].rearrange("p g r t -> p (g r t)"),
             )
 
-        def stage_h(dh):
-            for hl in range(2):
+        def stage_h(dh, hls=(0, 1)):
+            for hl in hls:
                 ps4 = psf.tile([P, 4, P], F32, tag="f", name="ps4")
                 for jl in range(4):
                     e0 = (4 * hl + jl) * P
                     nc.tensor.matmul(ps4[:, jl, :], lhsT=x3s[dh][:, e0 : e0 + P], rhs=g8[:], start=True, stop=True)
                 ps4s[(dh, hl)] = ps4
 
-        def stage_i(dh):
-            for hl in range(2):
+        def stage_i(dh, hls=(0, 1)):
+            for hl in hls:
                 nc.scalar.copy(
                     out=ut[:, dh, :, 4 * hl : 4 * hl + 4, :],
                     in_=ps4s[(dh, hl)][:].rearrange("p j (c n) -> p c j n", n=8),
@@ -198,7 +198,11 @@ def tile_waveletgatednet_w_kernel(tc, x, W_words, W_scales, b, threshold, out):
                     zn.append(zt[:])
                 zss[hc] = zn
             zs = zss[hc]
-            for g, jl in [(g, jl) for g in range(g0, g1) for jl in range(4)]:
+            if hc == 7:
+                order = [(g, jl) for g in range(g0, g1) for jl in range(4)]
+            else:
+                order = [(g, jl) for gp in range(g0, g1, 2) for jl in range(4) for g in (gp, gp + 1)]
+            for g, jl in order:
                 n0 = 512 * hc + P * jl
                 w0 = 512 * (hc % 2) + P * jl
                 nc.tensor.matmul_mx(
@@ -211,16 +215,15 @@ def tile_waveletgatednet_w_kernel(tc, x, W_words, W_scales, b, threshold, out):
                     stop=(g == 7),
                 )
 
-        def part(tile4, hc):
-            hl = hc % 2
-            return tile4[:, :, 4 * hl : 4 * hl + 4, :].rearrange("p c j n -> p c (j n)")
+        def part(tile4, j0, j1):
+            return tile4[:, :, j0:j1, :].rearrange("p c j n -> p c (j n)")
 
-        def sig(hc):
+        def sig(hc, jls=(0, 1, 2, 3)):
             dh = hc // 2
-            if hc % 2 == 0:
+            if dh not in gates:
                 gnew = ep.tile([P, 16, 8, 8], F32, name="gate")
                 gates[dh] = gnew
-            for jl in range(4):
+            for jl in jls:
                 eb = 4 * hc + jl
                 nc.scalar.activation(
                     out=gates[dh][:, :, 4 * (hc % 2) + jl, :],
@@ -230,24 +233,21 @@ def tile_waveletgatednet_w_kernel(tc, x, W_words, W_scales, b, threshold, out):
                     scale=1.0,
                 )
 
-        def prod(hc):
-            dh = hc // 2
-            if hc % 2 == 0:
+        def prod(dh, j0, j1):
+            if dh not in gts:
                 gtn = ep.tile([P, 16, 8, 8], F32, name="gt")
                 gts[dh] = gtn
-            nc.vector.tensor_tensor(out=part(gts[dh][:], hc), in0=part(gates[dh][:], hc), in1=part(ut[:, dh], hc), op=ALU.mult)
+            nc.vector.tensor_tensor(out=part(gts[dh][:], j0, j1), in0=part(gates[dh][:], j0, j1), in1=part(ut[:, dh], j0, j1), op=ALU.mult)
 
-        def square(hc):
-            dh = hc // 2
-            if hc % 2 == 0:
+        def square(dh, j0, j1):
+            if dh not in sqs:
                 sqn = ep.tile([P, 16, 8, 8], F32, name="sq")
                 sqs[dh] = sqn
-            nc.scalar.activation(out=part(sqs[dh][:], hc), in_=part(gts[dh][:], hc), func=ACT.Square)
+            nc.scalar.activation(out=part(sqs[dh][:], j0, j1), in_=part(gts[dh][:], j0, j1), func=ACT.Square)
 
-        def select(hc):
-            dh = hc // 2
+        def select(dh, j0, j1):
             nc.vector.scalar_tensor_tensor(
-                out=part(sqs[dh][:], hc), in0=part(sqs[dh][:], hc), scalar=tsq[:, 0:1], in1=part(gts[dh][:], hc), op0=ALU.is_ge, op1=ALU.mult
+                out=part(sqs[dh][:], j0, j1), in0=part(sqs[dh][:], j0, j1), scalar=tsq[:, 0:1], in1=part(gts[dh][:], j0, j1), op0=ALU.is_ge, op1=ALU.mult
             )
 
         def level1(dh, j0, j1):
@@ -320,38 +320,35 @@ def tile_waveletgatednet_w_kernel(tc, x, W_words, W_scales, b, threshold, out):
         stage_h(0)
         stage_i(0)
         mx(0, 6, 8)
-        for dh in range(4):
-            even = 2 * dh
-            odd = even + 1
-            sig(even)
-            prod(even)
-            square(even)
-            mx(odd, 0, 4)
-            if dh > 0:
-                back(dh - 1)
-            mx(odd, 4, 8)
-            if dh == 0:
+        for h in range(8):
+            dh = h // 2
+            j0 = 4 * (h % 2)
+            pd = (h - 1) // 2
+            pj = 4 * ((h - 1) % 2)
+            sig(h)
+            if h < 6:
+                stage_h((h + 2) // 2, (h % 2,))
+            if h >= 3 and h % 2 == 1:
+                back((h - 3) // 2)
+            if h < 7:
+                mx(h + 1)
+            if h == 0:
                 load_w(3)
-            if dh < 3:
-                stage_h(dh + 1)
-            if dh > 0:
-                fin(dh - 1, 0)
-                fin(dh - 1, 1)
-            select(even)
-            level1(dh, 0, 4)
-            sig(odd)
-            prod(odd)
-            square(odd)
-            if dh < 3:
-                stage_i(dh + 1)
-                mx(even + 2, 0, 4)
-                mx(even + 2, 4, 8)
-            level2(dh, 0, 4)
-            select(odd)
-            level3(dh, 0, 4)
-            level1(dh, 4, 8)
-            level2(dh, 4, 8)
-            level3(dh, 4, 8)
+            prod(dh, j0, j0 + 4)
+            if h < 6:
+                stage_i((h + 2) // 2, (h % 2,))
+            square(dh, j0, j0 + 4)
+            if h >= 1:
+                level2(pd, pj, pj + 4)
+            if h >= 3:
+                fin((h - 3) // 2, (h - 3) % 2)
+            select(dh, j0, j0 + 4)
+            if h >= 1:
+                level3(pd, pj, pj + 4)
+            level1(dh, j0, j0 + 4)
+        fin(2, 1)
+        level2(3, 4, 8)
+        level3(3, 4, 8)
         back(3)
         fin(3, 0)
         fin(3, 1)

@@ -270,12 +270,12 @@ def tile_waveletgatednet_w_kernel(tc, x, W_words, W_scales, b, threshold, out):
                     out=y2s[dh][:, bb, :, :, j0:j1, :].rearrange("p b c j r -> p b c (j r)"), in0=src[:, :, :, :, 0], in1=src[:, :, :, :, 1], op=op
                 )
 
-        def level3(dh, j0, j1):
+        def level3(dh, j0, j1, ops=ADD_SUB):
             if dh not in y3s:
                 y3n = ep.tile([P, 2, 4, 16, 8], F32, name="y3")
                 y3s[dh] = y3n
             src = y2s[dh][:, :, :, :, j0:j1, :].rearrange("p x b c j two -> p (x b) c j two")
-            for bb, op in ADD_SUB:
+            for bb, op in ops:
                 nc.vector.tensor_tensor(out=y3s[dh][:, bb, :, :, j0:j1], in0=src[:, :, :, :, 0], in1=src[:, :, :, :, 1], op=op)
 
         def back(dh):
@@ -286,15 +286,15 @@ def tile_waveletgatednet_w_kernel(tc, x, W_words, W_scales, b, threshold, out):
                     nc.tensor.transpose(po[:, il, :], y3p[:, h, il, :], ident_f[:])
                 pos[(dh, h)] = po
 
-        def fin(dh, h):
-            if h == 0:
+        def fin(dh, h, e0=0, e1=P):
+            if dh not in ots:
                 otn = fx.tile([P, P, 8], F32, name="ot")
                 ots[dh] = otn
             xr = xt[:, dh, :].rearrange("p (e i) -> p e i", i=8)
             nc.vector.tensor_tensor(
-                out=ots[dh][:, :, 4 * h : 4 * h + 4],
-                in0=pos[(dh, h)][:].rearrange("p i e -> p e i"),
-                in1=xr[:, :, 4 * h : 4 * h + 4],
+                out=ots[dh][:, e0:e1, 4 * h : 4 * h + 4],
+                in0=pos[(dh, h)][:, :, e0:e1].rearrange("p i e -> p e i"),
+                in1=xr[:, e0:e1, 4 * h : 4 * h + 4],
                 op=ALU.add,
             )
 
@@ -320,6 +320,11 @@ def tile_waveletgatednet_w_kernel(tc, x, W_words, W_scales, b, threshold, out):
         stage_h(0)
         stage_i(0)
         mx(0, 6, 8)
+        def keep_warm(src, n):
+            for rep_i in range(n):
+                junk = psz.tile([P, P], F32, tag="z", name="junk")
+                nc.tensor.matmul(junk[:], lhsT=ident_f[:], rhs=src, start=True, stop=True)
+
         for h in range(8):
             dh = h // 2
             j0 = 4 * (h % 2)
@@ -343,14 +348,24 @@ def tile_waveletgatednet_w_kernel(tc, x, W_words, W_scales, b, threshold, out):
             if h >= 3:
                 fin((h - 3) // 2, (h - 3) % 2)
             select(dh, j0, j0 + 4)
-            if h >= 1:
+            if h == 7:
+                keep_warm(sqs[3][:, 0:4, 4:8, :].rearrange("p c j n -> p c (j n)"), 2)
+            if 1 <= h < 7:
                 level3(pd, pj, pj + 4)
+            if h == 7:
+                level3(pd, pj, pj + 4, ADD_SUB[0:1])
             level1(dh, j0, j0 + 4)
-        fin(2, 1)
+            if h == 7:
+                level3(pd, pj, pj + 4, ADD_SUB[1:2])
+                keep_warm(y1s[3][:, 1, 0:8, 4:8, :].rearrange("p c j r -> p c (j r)"), 2)
         level2(3, 4, 8)
         level3(3, 4, 8)
         back(3)
+        fin(2, 1)
         fin(3, 0)
-        fin(3, 1)
-        for dh in range(4):
+        for dh in range(3):
             nc.sync.dma_start(out=ov[:, :, dh, :], in_=ots[dh][:].rearrange("p e i -> p (e i)"))
+        fin(3, 1, 0, 64)
+        nc.sync.dma_start(out=ov[:, :, 3, 0:512], in_=ots[3][:, 0:64, :].rearrange("p e i -> p (e i)"))
+        fin(3, 1, 64, P)
+        nc.scalar.dma_start(out=ov[:, :, 3, 512:1024], in_=ots[3][:, 64:P, :].rearrange("p e i -> p (e i)"))

@@ -320,12 +320,13 @@ def tile_waveletgatednet_w_kernel(tc, x, W_words, W_scales, b, threshold, out):
         stage_h(0)
         stage_i(0)
         mx(0, 6, 8)
+
         def keep_warm(src, n):
             for rep_i in range(n):
                 junk = psz.tile([P, P], F32, tag="z", name="junk")
                 nc.tensor.matmul(junk[:], lhsT=ident_f[:], rhs=src, start=True, stop=True)
 
-        for h in range(8):
+        for h in range(7):
             dh = h // 2
             j0 = 4 * (h % 2)
             pd = (h - 1) // 2
@@ -335,8 +336,7 @@ def tile_waveletgatednet_w_kernel(tc, x, W_words, W_scales, b, threshold, out):
                 stage_h((h + 2) // 2, (h % 2,))
             if h >= 3 and h % 2 == 1:
                 back((h - 3) // 2)
-            if h < 7:
-                mx(h + 1)
+            mx(h + 1)
             if h == 0:
                 load_w(3)
             prod(dh, j0, j0 + 4)
@@ -348,20 +348,30 @@ def tile_waveletgatednet_w_kernel(tc, x, W_words, W_scales, b, threshold, out):
             if h >= 3:
                 fin((h - 3) // 2, (h - 3) % 2)
             select(dh, j0, j0 + 4)
-            if h == 7:
-                keep_warm(sqs[3][:, 0:4, 4:8, :].rearrange("p c j n -> p c (j n)"), 2)
-            if 1 <= h < 7:
+            if h >= 1:
                 level3(pd, pj, pj + 4)
-            if h == 7:
-                level3(pd, pj, pj + 4, ADD_SUB[0:1])
             level1(dh, j0, j0 + 4)
-            if h == 7:
-                level3(pd, pj, pj + 4, ADD_SUB[1:2])
-                keep_warm(y1s[3][:, 1, 0:8, 4:8, :].rearrange("p c j r -> p c (j r)"), 2)
+        level2(3, 0, 4)
+        sig(7, (0, 1))
+        back(2)
+        prod(3, 4, 6)
+        sig(7, (2, 3))
+        prod(3, 6, 8)
+        square(3, 4, 6)
+        fin(2, 0)
+        square(3, 6, 8)
+        select(3, 4, 6)
+        select(3, 6, 8)
+        keep_warm(sqs[3][:, 0:4, 4:8, :].rearrange("p c j n -> p c (j n)"), 2)
+        level3(3, 0, 4, ADD_SUB[0:1])
+        level1(3, 4, 8)
+        level3(3, 0, 4, ADD_SUB[1:2])
+        keep_warm(y1s[3][:, 1, 0:8, 4:8, :].rearrange("p c j r -> p c (j r)"), 2)
         level2(3, 4, 8)
+        fin(2, 1, 0, 64)
         level3(3, 4, 8)
         back(3)
-        fin(2, 1)
+        fin(2, 1, 64, P)
         fin(3, 0)
         for dh in range(3):
             nc.sync.dma_start(out=ov[:, :, dh, :], in_=ots[dh][:].rearrange("p e i -> p (e i)"))

@@ -363,15 +363,15 @@ def tile_waveletgatednet_w_kernel(tc, x, W_words, W_scales, b, threshold, out):
         select(3, 4, 6)
         select(3, 6, 8)
         keep_warm(sqs[3][:, 0:4, 4:8, :].rearrange("p c j n -> p c (j n)"), 2)
-        level3(3, 0, 4, ADD_SUB[0:1])
+        fin(2, 1, 0, 64)
         level1(3, 4, 8)
-        level3(3, 0, 4, ADD_SUB[1:2])
+        fin(2, 1, 64, P)
         keep_warm(y1s[3][:, 1, 0:8, 4:8, :].rearrange("p c j r -> p c (j r)"), 2)
         level2(3, 4, 8)
-        fin(2, 1, 0, 64)
+        level3(3, 0, 4, ADD_SUB[0:1])
         level3(3, 4, 8)
+        level3(3, 0, 4, ADD_SUB[1:2])
         back(3)
-        fin(2, 1, 64, P)
         fin(3, 0)
         for dh in range(3):
             nc.sync.dma_start(out=ov[:, :, dh, :], in_=ots[dh][:].rearrange("p e i -> p (e i)"))

import math
from contextlib import ExitStack

import concourse.mybir as mybir
from concourse.masks import make_identity

F32 = mybir.dt.float32
BF16 = mybir.dt.bfloat16
I32 = mybir.dt.int32
U32 = mybir.dt.uint32
U8 = mybir.dt.uint8
FP8X4 = mybir.dt.float8_e4m3fn_x4
ALU = mybir.AluOpType
ACT = mybir.ActivationFunctionType

P = 128
D = 4096
FLOPS = 2 * 128 * 4096 * 4096


def tile_waveletgatednet_w_kernel(tc, x, W_words, W_scales, b, threshold, out):
    nc = tc.nc
    with ExitStack() as ctx:
        const = ctx.enter_context(tc.tile_pool(name="const", bufs=1))
        keep = ctx.enter_context(tc.tile_pool(name="keep", bufs=1))
        fw = ctx.enter_context(tc.tile_pool(name="fw", bufs=2))
        fx = ctx.enter_context(tc.tile_pool(name="fx", bufs=4))
        ep = ctx.enter_context(tc.tile_pool(name="ep", bufs=2))
        e1 = ctx.enter_context(tc.tile_pool(name="e1", bufs=1))
        wp = ctx.enter_context(tc.tile_pool(name="wp", bufs=3))
        psz = ctx.enter_context(tc.psum_pool(name="psz", bufs=4))
        pso = ctx.enter_context(tc.psum_pool(name="pso", bufs=2))
        psf = ctx.enter_context(tc.psum_pool(name="psf", bufs=2))
        ctx.enter_context(tc.manual_schedule())

        planes = keep.tile([P, 2, D], U8, align_bytes=64)
        xt = keep.tile([P, 4, 1024], BF16)
        cw = keep.tile([P, 8, P], U32, align_bytes=64)
        cs = keep.tile([P, 8, P], U8, align_bytes=64)
        ut = keep.tile([P, 4, 16, 8, 8], F32)

        nc.vector.memset(planes[:, 0, :].bitcast(I32), 0)
        btile = const.tile([P, P], BF16)
        nc.vector.memset(btile[:], 0.0)
        warm = const.tile([P, 1], F32)
        nc.vector.memset(warm[:], 0.0)

        xv = x.rearrange("o c (h j w) -> (o c) j h w", h=4, j=8)
        ov = out.rearrange("o c (h j w) -> (o c) j h w", h=4, j=8)
        for dh in range(4):
            nc.sync.dma_start(out=xt[:, dh, :], in_=xv[:, :, dh, :])
        nc.scalar.dma_start(out=btile[0:32, :], in_=b.rearrange("(r c) -> r c", c=P))
        thr_b = const.tile([P, 1], BF16)
        nc.scalar.dma_start(out=thr_b[:], in_=threshold.partition_broadcast(P))
        warm2 = const.tile([P, 1], F32)
        nc.scalar.activation(out=warm2[:], in_=warm[:], func=ACT.Sigmoid)
        row_i = const.tile([P, P], I32)
        nc.gpsimd.iota(row_i[:], pattern=[[0, P]], base=0, channel_multiplier=1)
        col_i = const.tile([P, P], I32)
        nc.gpsimd.iota(col_i[:], pattern=[[1, P]], base=0, channel_multiplier=0)
        ident_f = const.tile([P, P], F32)
        make_identity(nc, ident_f[:])
        nc.gpsimd.memset(planes[:, 1, :].bitcast(F32), 0.0)
        ident_b = const.tile([P, P], BF16)
        make_identity(nc, ident_b[:])
        for a in range(2):
            for q in (0, 2, 1, 3):
                nc.sync.dma_start(
                    out=planes[32 * q : 32 * q + 16, a, :].bitcast(I32),
                    in_=W_scales[4 * a : 4 * a + 4, 4 * q : 4 * q + 4, :].bitcast(I32),
                )
        w32 = W_words.rearrange("g p n t -> g p (n t)").bitcast(I32)
        wts = {}

        def load_w(dh):
            wt = wp.tile([P, 8, 1024], U32, align_bytes=64, name="wt")
            wts[dh] = wt
            for hl in range(2):
                c0 = 1024 * dh + 512 * hl
                if dh < 3 or hl == 0:
                    for gp in range(4):
                        nc.sync.dma_start(
                            out=wt[:, 2 * gp : 2 * gp + 2, 512 * hl : 512 * hl + 512].bitcast(I32),
                            in_=w32[2 * gp : 2 * gp + 2, :, c0 : c0 + 512].rearrange("g p n -> p g n"),
                        )
                else:
                    for g in range(8):
                        nc.sync.dma_start(out=wt[:, g, 512:1024].bitcast(I32), in_=w32[g, :, c0 : c0 + 512])

        for dh in range(3):
            load_w(dh)

        both = const.tile([P, P], I32)
        nc.vector.tensor_tensor(out=both[:], in0=row_i[:], in1=col_i[:], op=ALU.bitwise_and)
        sh1 = const.tile([P, P], I32)
        nc.vector.tensor_single_scalar(out=sh1[:], in_=both[:], scalar=1, op=ALU.logical_shift_right)
        sh2 = const.tile([P, P], I32)
        nc.vector.tensor_single_scalar(out=sh2[:], in_=both[:], scalar=2, op=ALU.logical_shift_right)
        nc.vector.tensor_tensor(out=sh1[:], in0=sh1[:], in1=both[:], op=ALU.bitwise_xor)
        nc.vector.tensor_tensor(out=sh1[:], in0=sh1[:], in1=sh2[:], op=ALU.bitwise_xor)
        nc.vector.tensor_single_scalar(out=sh1[:], in_=sh1[:], scalar=1, op=ALU.bitwise_and)
        diff = const.tile([P, P], I32)
        nc.vector.tensor_tensor(out=diff[:], in0=row_i[:], in1=col_i[:], op=ALU.bitwise_xor)
        nc.vector.tensor_single_scalar(out=diff[:], in_=diff[:], scalar=3, op=ALU.logical_shift_right)
        same = const.tile([P, P], F32)
        nc.vector.tensor_single_scalar(out=same[:], in_=diff[:], scalar=0, op=ALU.is_equal)
        sign = const.tile([P, P], F32)
        nc.vector.tensor_scalar(out=sign[:], in0=sh1[:], scalar1=-0.25, scalar2=0.125, op0=ALU.mult, op1=ALU.add)
        g8 = const.tile([P, P], BF16)
        nc.vector.tensor_tensor(out=g8[:], in0=same[:], in1=sign[:], op=ALU.mult)
        tsq = const.tile([P, 1], F32)
        bt = const.tile([P, 32], F32)

        xw = xt[:].rearrange("p h w -> p (h w)").bitcast(F32)
        ps1s = {}
        rws = {}
        ps2s = {}
        x3s = {}
        ps3s = {}
        grps = {}
        ps4s = {}

        def stage_a(dh):
            ps1 = psf.tile([P, 4, P], F32, tag="f", name="ps1")
            for m in range(4):
                nc.tensor.transpose(ps1[:, m, :], xw[:, 512 * dh + m : 512 * (dh + 1) : 4], ident_f[:])
            ps1s[dh] = ps1

        def stage_b(dh):
            rw = fw.tile([P, 8, 16, 4], F32, name="rw")
            nc.scalar.copy(out=rw[:], in_=ps1s[dh][:].rearrange("p m (c j) -> p j c m", j=8))
            rws[dh] = rw

        def stage_c(dh):
            rb = rws[dh][:].rearrange("p j c m -> p j (c m)").bitcast(BF16)
            ps2 = psf.tile([P, 8, P], BF16, tag="f", name="ps2")
            for jj in range(8):
                nc.tensor.transpose(ps2[:, jj, :], rb[:, jj, :], ident_b[:])
            ps2s[dh] = ps2

        def stage_d(dh):
            x3 = fx.tile([P, 1024], BF16, name="x3")
            nc.vector.tensor_copy(out=x3[:], in_=ps2s[dh][:].rearrange("p j e -> p (j e)"))
            x3s[dh] = x3

        def stage_e(dh):
            for gl in range(2):
                ps3 = pso.tile([P, 4, P], F32, tag="o", name="ps3")
                for t in range(4):
                    nc.tensor.matmul(ps3[:, t, :], lhsT=x3s[dh][:, 512 * gl + t : 512 * (gl + 1) : 4], rhs=g8[:], start=True, stop=True)
                ps3s[(dh, gl)] = ps3

        def stage_f(dh):
            grp = fw.tile([P, 2, P, 4], BF16, align_bytes=64, name="grp")
            nc.scalar.activation(out=grp[:, 0], in_=ps3s[(dh, 0)][:].rearrange("p t r -> p r t"), func=ACT.Copy, scale=math.sqrt(8.0))
            nc.vector.tensor_single_scalar(out=grp[:, 1], in_=ps3s[(dh, 1)][:].rearrange("p t r -> p r t"), scalar=math.sqrt(8.0), op=ALU.mult)
            grps[dh] = grp

        def stage_q(dh):
            nc.vector.quantize_mx(
                out=cw[:, 2 * dh : 2 * dh + 2, :].rearrange("p g r -> p (g r)").bitcast(FP8X4),
                scales=cs[:, 2 * dh : 2 * dh + 2, :].rearrange("p g r -> p (g r)"),
                in_=grps[dh][:].rearrange("p g r t -> p (g r t)"),
            )

        def stage_h(dh, hls=(0, 1)):
            for hl in hls:
                ps4 = psf.tile([P, 4, P], F32, tag="f", name="ps4")
                for jl in range(4):
                    e0 = (4 * hl + jl) * P
                    nc.tensor.matmul(ps4[:, jl, :], lhsT=x3s[dh][:, e0 : e0 + P], rhs=g8[:], start=True, stop=True)
                ps4s[(dh, hl)] = ps4

        def stage_i(dh, hls=(0, 1)):
            for hl in hls:
                nc.scalar.copy(
                    out=ut[:, dh, :, 4 * hl : 4 * hl + 4, :],
                    in_=ps4s[(dh, hl)][:].rearrange("p j (c n) -> p c j n", n=8),
                )


        zss = {}
        gates = {}
        gts = {}
        sqs = {}
        y1s = {}
        y2s = {}
        y3s = {}
        pos = {}
        ots = {}
        ADD_SUB = ((0, ALU.add), (1, ALU.subtract))

        def mx(hc, g0=0, g1=8):
            if g0 == 0:
                zn = []
                for jl in range(4):
                    zt = psz.tile([P, P], F32, tag="z", name="zt")
                    zn.append(zt[:])
                zss[hc] = zn
            zs = zss[hc]
            if hc == 7:
                order = [(g, jl) for g in range(g0, g1) for jl in range(4)]
            else:
                order = [(g, jl) for gp in range(g0, g1, 2) for jl in range(4) for g in (gp, gp + 1)]
            for g, jl in order:
                n0 = 512 * hc + P * jl
                w0 = 512 * (hc % 2) + P * jl
                nc.tensor.matmul_mx(
                    out=zs[jl],
                    lhsT=wts[hc // 2][:, g, w0 : w0 + P].bitcast(FP8X4),
                    lhsT_scale=planes[4 * (g % 4) : P, g // 4, n0 : n0 + P],
                    rhs=cw[:, g, :].bitcast(FP8X4),
                    rhs_scale=cs[:, g, :],
                    start=(g == 0),
                    stop=(g == 7),
                )

        def part(tile4, j0, j1):
            return tile4[:, :, j0:j1, :].rearrange("p c j n -> p c (j n)")

        def sig(hc, jls=(0, 1, 2, 3)):
            dh = hc // 2
            if dh not in gates:
                gnew = ep.tile([P, 16, 8, 8], F32, name="gate")
                gates[dh] = gnew
            for jl in jls:
                eb = 4 * hc + jl
                nc.scalar.activation(
                    out=gates[dh][:, :, 4 * (hc % 2) + jl, :],
                    in_=zss[hc][jl].rearrange("p (c n) -> p c n", n=8),
                    func=ACT.Sigmoid,
                    bias=bt[:, eb : eb + 1],
                    scale=1.0,
                )

        def prod(dh, j0, j1):
            if dh not in gts:
                gtn = ep.tile([P, 16, 8, 8], F32, name="gt")
                gts[dh] = gtn
            nc.vector.tensor_tensor(out=part(gts[dh][:], j0, j1), in0=part(gates[dh][:], j0, j1), in1=part(ut[:, dh], j0, j1), op=ALU.mult)

        def square(dh, j0, j1):
            if dh not in sqs:
                sqn = ep.tile([P, 16, 8, 8], F32, name="sq")
                sqs[dh] = sqn
            nc.scalar.activation(out=part(sqs[dh][:], j0, j1), in_=part(gts[dh][:], j0, j1), func=ACT.Square)

        def select(dh, j0, j1):
            nc.vector.scalar_tensor_tensor(
                out=part(sqs[dh][:], j0, j1), in0=part(sqs[dh][:], j0, j1), scalar=tsq[:, 0:1], in1=part(gts[dh][:], j0, j1), op0=ALU.is_ge, op1=ALU.mult
            )

        def level1(dh, j0, j1):
            if dh not in y1s:
                y1n = e1.tile([P, 2, 16, 8, 4], F32, name="y1")
                y1s[dh] = y1n
            src = sqs[dh][:, :, j0:j1, :].rearrange("p c j (r two) -> p c (j r) two", two=2)
            for bb, op in ADD_SUB:
                nc.vector.tensor_tensor(
                    out=y1s[dh][:, bb, :, j0:j1, :].rearrange("p c j r -> p c (j r)"), in0=src[:, :, :, 0], in1=src[:, :, :, 1], op=op
                )

        def level2(dh, j0, j1):
            if dh not in y2s:
                y2n = e1.tile([P, 2, 2, 16, 8, 2], F32, name="y2")
                y2s[dh] = y2n
            src = y1s[dh][:, :, :, j0:j1, :].rearrange("p b c j (r two) -> p b c (j r) two", two=2)
            for bb, op in ADD_SUB:
                nc.vector.tensor_tensor(
                    out=y2s[dh][:, bb, :, :, j0:j1, :].rearrange("p b c j r -> p b c (j r)"), in0=src[:, :, :, :, 0], in1=src[:, :, :, :, 1], op=op
                )

        def level3(dh, j0, j1, ops=ADD_SUB):
            if dh not in y3s:
                y3n = ep.tile([P, 2, 4, 16, 8], F32, name="y3")
                y3s[dh] = y3n
            src = y2s[dh][:, :, :, :, j0:j1, :].rearrange("p x b c j two -> p (x b) c j two")
            for bb, op in ops:
                nc.vector.tensor_tensor(out=y3s[dh][:, bb, :, :, j0:j1], in0=src[:, :, :, :, 0], in1=src[:, :, :, :, 1], op=op)

        def back(dh):
            y3p = y3s[dh][:].rearrange("p h i c j -> p h i (c j)")
            for h in range(2):
                po = pso.tile([P, 4, P], F32, tag="o", name="po")
                for il in range(4):
                    nc.tensor.transpose(po[:, il, :], y3p[:, h, il, :], ident_f[:])
                pos[(dh, h)] = po

        def fin(dh, h, e0=0, e1=P):
            if dh not in ots:
                otn = fx.tile([P, P, 8], F32, name="ot")
                ots[dh] = otn
            xr = xt[:, dh, :].rearrange("p (e i) -> p e i", i=8)
            nc.vector.tensor_tensor(
                out=ots[dh][:, e0:e1, 4 * h : 4 * h + 4],
                in0=pos[(dh, h)][:, :, e0:e1].rearrange("p i e -> p e i"),
                in1=xr[:, e0:e1, 4 * h : 4 * h + 4],
                op=ALU.add,
            )

        for s in range(7):
            if s < 4:
                stage_a(s)
                stage_b(s)
            if 0 <= s - 3 < 4:
                stage_q(s - 3)
            if 0 <= s - 1 < 4:
                stage_c(s - 1)
                stage_d(s - 1)
            if 0 <= s - 2 < 4:
                stage_e(s - 2)
                stage_f(s - 2)
            if s == 3:
                psb = pso.tile([P, P], BF16, tag="o", name="psb")
                nc.tensor.transpose(psb[:], btile[:], ident_b[:])
                nc.vector.tensor_copy(out=bt[:], in_=psb[:, 0:32])
                nc.vector.scalar_tensor_tensor(out=tsq[:], in0=thr_b[:], scalar=0.125, in1=thr_b[:], op0=ALU.mult, op1=ALU.mult)
            if s >= 4:
                mx(0, 2 * (s - 4), 2 * (s - 4) + 2)
        stage_h(0)
        stage_i(0)
        mx(0, 6, 8)

        def keep_warm(src, n):
            for rep_i in range(n):
                junk = psz.tile([P, P], F32, tag="z", name="junk")
                nc.tensor.matmul(junk[:], lhsT=ident_f[:], rhs=src, start=True, stop=True)

        for h in range(7):
            dh = h // 2
            j0 = 4 * (h % 2)
            pd = (h - 1) // 2
            pj = 4 * ((h - 1) % 2)
            sig(h)
            if h < 6:
                stage_h((h + 2) // 2, (h % 2,))
            if h >= 3 and h % 2 == 1:
                back((h - 3) // 2)
            mx(h + 1)
            if h == 0:
                load_w(3)
            prod(dh, j0, j0 + 4)
            if h < 6:
                stage_i((h + 2) // 2, (h % 2,))
            square(dh, j0, j0 + 4)
            if h >= 1:
                level2(pd, pj, pj + 4)
            if h >= 3:
                fin((h - 3) // 2, (h - 3) % 2)
            select(dh, j0, j0 + 4)
            if h >= 1:
                level3(pd, pj, pj + 4)
            level1(dh, j0, j0 + 4)
        level2(3, 0, 4)
        sig(7, (0, 1))
        back(2)
        prod(3, 4, 6)
        sig(7, (2, 3))
        prod(3, 6, 8)
        square(3, 4, 6)
        fin(2, 0)
        square(3, 6, 8)
        select(3, 4, 6)
        select(3, 6, 8)
        keep_warm(sqs[3][:, 0:4, 4:8, :].rearrange("p c j n -> p c (j n)"), 2)
        fin(2, 1, 0, 64)
        level1(3, 4, 8)
        fin(2, 1, 64, P)
        keep_warm(y1s[3][:, 1, 0:8, 4:8, :].rearrange("p c j r -> p c (j r)"), 2)
        level2(3, 4, 8)
        level3(3, 0, 4, ADD_SUB[0:1])
        level3(3, 4, 8)
        level3(3, 0, 4, ADD_SUB[1:2])
        back(3)
        fin(3, 0)
        for dh in range(3):
            nc.sync.dma_start(out=ov[:, :, dh, :], in_=ots[dh][:].rearrange("p e i -> p (e i)"))
        fin(3, 1, 0, 64)
        nc.sync.dma_start(out=ov[:, :, 3, 0:512], in_=ots[3][:, 0:64, :].rearrange("p e i -> p (e i)"))
        fin(3, 1, 64, P)
        nc.scalar.dma_start(out=ov[:, :, 3, 512:1024], in_=ots[3][:, 64:P, :].rearrange("p e i -> p (e i)"))
